import numpy as np
import ml_dtypes


def mxq(x, axis, fmt="e4m3"):
    dtype, down = {"e4m3": (ml_dtypes.float8_e4m3fn, 7), "e5m2": (ml_dtypes.float8_e5m2, 14)}[fmt]
    v = np.moveaxis(np.asarray(x, np.float32).astype(ml_dtypes.bfloat16).astype(np.float64), axis, -1)
    blocks = v.reshape(v.shape[:-1] + (-1, 32))
    amax = np.abs(blocks).max(-1, keepdims=True)
    byte = np.maximum(np.where(amax > 0, np.frexp(amax)[1] - 1 + 127, 0) - down, 1)
    scale = np.exp2(byte - 127.0)
    codes = (blocks / scale).astype(np.float32).astype(dtype).astype(np.float64)
    return np.moveaxis((codes * scale).reshape(v.shape), -1, axis)


WIDE = False


def mx_kscale(k):
    if not WIDE:
        return np.ones(k)
    levels = np.array([10, -10, 5, -5, 0])
    a = np.random.permutation(np.resize(levels, k // 512 * 4)).reshape(k // 512, 4)
    idx = np.arange(k)
    return np.exp2(a[idx // 512, idx % 128 // 32])


BF16 = ml_dtypes.bfloat16


def bf(x):
    return np.asarray(x, np.float32).astype(BF16)


def f64(x):
    return np.asarray(x).astype(np.float64)


B, S, D, H, DFF = 4, 256, 512, 8, 2048


def wave(v, w1, w2):
    return w1 * np.sin(v) + w2 * np.cos(v)


def setup_inputs():
    n = np.random.standard_normal
    s = mx_kscale(DFF)
    u = n((B, S, DFF))
    return {
        "h1": bf((np.sin(u) + np.cos(u)) * s),
        "x1": bf(n((B, S, D)) * 1.2),
        "ffn_w2": bf(n((DFF, DFF)) / np.sqrt(DFF) / s[None, :]),
        "ffn_b2": bf(n(DFF) * 0.2),
        "ffn_a2w1": bf(1.2 + 0.1 * n(1)),
        "ffn_a2w2": bf(0.8 + 0.1 * n(1)),
        "ffn_w3": bf(n((D, DFF)) / np.sqrt(DFF)),
        "ffn_b3": bf(n(D) * 0.2),
    }


def reference(h1, x1, ffn_w2, ffn_b2, ffn_a2w1, ffn_a2w2, ffn_w3, ffn_b3):
    u2 = (mxq(f64(h1), 2, "e4m3") @ mxq(f64(ffn_w2), 1, "e4m3").T) + f64(ffn_b2)
    h2 = wave(u2, f64(ffn_a2w1), f64(ffn_a2w2))
    ffn_out = (mxq(h2, 2, "e4m3") @ mxq(f64(ffn_w3), 1, "e4m3").T) + f64(ffn_b3)
    return f64(x1) + ffn_out

@@ -1,0 +1,345 @@
+import math
+from contextlib import ExitStack
+
+import concourse.mybir as mybir
+from concourse.masks import make_identity
+
+F32 = mybir.dt.float32
+BF16 = mybir.dt.bfloat16
+I32 = mybir.dt.int32
+U32 = mybir.dt.uint32
+U8 = mybir.dt.uint8
+FP8X4 = mybir.dt.float8_e4m3fn_x4
+ALU = mybir.AluOpType
+ACT = mybir.ActivationFunctionType
+
+P = 128
+PACK = 4
+K_PASS = P * PACK
+TOKENS = 1024
+D_FF = 2048
+D_MODEL = 512
+PASSES = D_FF // K_PASS
+HALF = 512
+HALVES = TOKENS // HALF
+ROW_TILES = 2
+CHUNK_ROWS = ROW_TILES * P
+WORDS = D_FF // 2
+FEATURE_TILES = D_FF // P
+W2_CHUNKS = D_FF // CHUNK_ROWS
+TOKEN_TILES = TOKENS // P
+TILES_PER_HALF = HALF // P
+RAW_BUFS = 6
+NEWTON_STEPS = 3
+TWO_PI = 2.0 * math.pi
+HALF_PI = 0.5 * math.pi
+TINY = 1e-36
+
+FLOPS = 2 * TOKENS * D_FF * D_FF + 2 * TOKENS * D_FF * D_MODEL
+
+
+def tile_transreachencoderlayer_pb_kernel(
+    tc, h1, x1, ffn_w2, ffn_b2, ffn_a2w1, ffn_a2w2, ffn_w3, ffn_b3, out
+):
+    nc = tc.nc
+    h1_rows = h1.rearrange("b s k -> (b s) k")
+    x1_rows = x1.rearrange("b s d -> (b s) d")
+    out_rows = out.rearrange("b s d -> (b s) d")
+
+    with ExitStack() as ctx:
+        keep = ctx.enter_context(tc.tile_pool(name="keep", bufs=1))
+        raw_pool = ctx.enter_context(tc.tile_pool(name="raw", bufs=RAW_BUFS))
+        grouped_pool = ctx.enter_context(tc.tile_pool(name="grouped", bufs=3))
+        turns_pool = ctx.enter_context(tc.tile_pool(name="turns", bufs=2))
+        angle_pool = ctx.enter_context(tc.tile_pool(name="angle", bufs=3))
+        h2_pool = ctx.enter_context(tc.tile_pool(name="h2", bufs=2))
+        bank_pool = ctx.enter_context(tc.psum_pool(name="bank", bufs=4))
+        sums_pool = ctx.enter_context(tc.psum_pool(name="sums", bufs=4))
+        ctx.enter_context(tc.manual_schedule())
+
+        h1_codes = keep.tile([P, HALVES, PASSES, HALF], U32, align_bytes=64)
+        h1_scales = keep.tile([P, HALVES, PASSES, HALF], U8, align_bytes=64)
+        w2_codes = keep.tile([P, FEATURE_TILES, PASSES, P], U32, align_bytes=64)
+        w2_scales = keep.tile([P, FEATURE_TILES, PASSES, P], U8, align_bytes=64)
+        w3_codes = keep.tile([P, PASSES, D_MODEL], U32, align_bytes=64)
+        w3_scales = keep.tile([P, PASSES, D_MODEL], U8, align_bytes=64)
+        h2_codes = keep.tile([P, HALVES, PASSES, HALF], U32, align_bytes=64)
+        h2_scales = keep.tile([P, HALVES, PASSES, HALF], U8, align_bytes=64)
+
+        identity = keep.tile([P, P], F32)
+        make_identity(nc, identity[:])
+
+        chunks = (
+            [("h1", c) for c in range(2)]
+            + [("w2", c) for c in range(W2_CHUNKS)]
+            + [("h1", c) for c in range(2, 4)]
+            + [("w3", c) for c in range(2)]
+        )
+        raw_tiles = {}
+        residual = keep.tile([P, TOKEN_TILES, D_MODEL], F32)
+        b3_rows = keep.tile([P, D_MODEL], BF16)
+
+        def load_chunk(i):
+            kind, c = chunks[i]
+            rows = slice(c * CHUNK_ROWS, (c + 1) * CHUNK_ROWS)
+            raw = raw_pool.tile([P, ROW_TILES, D_FF], BF16, tag="raw")
+            if kind == "h1":
+                source = h1_rows[rows, :].rearrange("(r p) k -> p r k", p=P)
+            elif kind == "w3":
+                source = ffn_w3[rows, :].rearrange("(r p) k -> p r k", p=P)
+            else:
+                source = ffn_w2[rows, :].rearrange("(p r) k -> p r k", p=P)
+            nc.sync.dma_start(out=raw[:], in_=source)
+            raw_tiles[i] = raw
+
+        def load_residual():
+            x1_raw = raw_pool.tile([P, TOKEN_TILES, D_MODEL], BF16, tag="raw")
+            nc.sync.dma_start(out=b3_rows[:], in_=ffn_b3.partition_broadcast(P))
+            nc.sync.dma_start(out=x1_raw[:], in_=x1_rows.rearrange("(t p) d -> p t d", p=P))
+            for t in range(TOKEN_TILES):
+                nc.gpsimd.tensor_tensor(
+                    out=residual[:, t, :], in0=x1_raw[:, t, :], in1=b3_rows[:], op=ALU.add
+                )
+
+        def load(i):
+            if i < len(chunks):
+                load_chunk(i)
+            elif i == len(chunks):
+                load_residual()
+
+        next_chunk = [0]
+
+        def prepare_next():
+            i = next_chunk[0]
+            next_chunk[0] = i + 1
+            kind, c = chunks[i]
+            words = raw_tiles[i][:].rearrange("p r k -> p (r k)").bitcast(F32)
+            grouped = grouped_pool.tile([P, ROW_TILES * D_FF], BF16, align_bytes=64)
+            grouped_words = grouped[:].bitcast(F32)
+            if kind == "w2":
+                target = grouped_words.rearrange(
+                    "p (r k i u) -> p r k i u", r=ROW_TILES, k=PASSES, i=P
+                )
+            else:
+                target = grouped_words.rearrange(
+                    "p (k r i u) -> p k r i u", r=ROW_TILES, k=PASSES, i=P
+                )
+            for r in range(ROW_TILES):
+                for j in range(PASSES // 2):
+                    bank = bank_pool.tile([P, 2, 2, P], F32, tag="bank")
+                    for k in range(2):
+                        for u in range(2):
+                            first = r * WORDS + ((2 * j + k) * 2 + u) * P
+                            nc.tensor.transpose(
+                                bank[:, k, u, :], words[:, first : first + P], identity[:]
+                            )
+                    passes = slice(2 * j, 2 * j + 2)
+                    nc.scalar.copy(
+                        out=target[:, r, passes, :, :] if kind == "w2" else target[:, passes, r, :, :],
+                        in_=bank[:].rearrange("q k u i -> q k i u"),
+                    )
+            load(i + RAW_BUFS)
+            if kind == "w2":
+                tiles = slice(ROW_TILES * c, ROW_TILES * (c + 1))
+                nc.vector.quantize_mx(
+                    out=w2_codes[:, tiles, :, :].rearrange("p m k o -> p (m k o)").bitcast(FP8X4),
+                    scales=w2_scales[:, tiles, :, :].rearrange("p m k o -> p (m k o)"),
+                    in_=grouped[:],
+                )
+                return
+            for k in range(PASSES):
+                if kind == "h1":
+                    half, part = divmod(c, HALF // CHUNK_ROWS)
+                    cols = slice(part * CHUNK_ROWS, (part + 1) * CHUNK_ROWS)
+                    codes, scales = h1_codes[:, half, k, cols], h1_scales[:, half, k, cols]
+                else:
+                    cols = slice(c * CHUNK_ROWS, (c + 1) * CHUNK_ROWS)
+                    codes, scales = w3_codes[:, k, cols], w3_scales[:, k, cols]
+                nc.vector.quantize_mx(
+                    out=codes.bitcast(FP8X4),
+                    scales=scales,
+                    in_=grouped[:, k * CHUNK_ROWS * PACK : (k + 1) * CHUNK_ROWS * PACK],
+                )
+
+        a_bf = keep.tile([P, 1], BF16)
+        b_bf = keep.tile([P, 1], BF16)
+        b2_bf = keep.tile([P, FEATURE_TILES], BF16)
+        gains = keep.tile([P, 2], F32)
+        sign_a = keep.tile([P, 1], F32)
+        squares = keep.tile([P, 2], F32)
+        norm2 = keep.tile([P, 1], F32)
+        minus_half = keep.tile([P, 1], F32)
+        inv_norm = keep.tile([P, 1], F32)
+        cos_sin = keep.tile([P, 2], F32)
+        gain = keep.tile([P, 1], F32)
+        phase = keep.tile([P, 2], F32)
+        sin_cos_now = keep.tile([P, 2], F32)
+        step = keep.tile([P, 1], F32)
+        bias = keep.tile([P, FEATURE_TILES], F32)
+        bias_turns = keep.tile([P, FEATURE_TILES], F32)
+
+        def wave_constants():
+            nc.scalar.dma_start(out=a_bf[:], in_=ffn_a2w1.partition_broadcast(P))
+            nc.scalar.dma_start(out=b_bf[:], in_=ffn_a2w2.partition_broadcast(P))
+            nc.scalar.dma_start(
+                out=b2_bf[:].rearrange("p (c e) -> p c e", e=2),
+                in_=ffn_b2.rearrange("(c p e) -> p c e", p=P, e=2),
+            )
+            nc.vector.memset(minus_half[:], -0.5)
+            nc.scalar.activation(out=step[:], in_=minus_half[:], func=ACT.Sin)
+            nc.vector.tensor_copy(out=gains[:, 0:1], in_=a_bf[:])
+            nc.vector.tensor_copy(out=gains[:, 1:2], in_=b_bf[:])
+            nc.vector.tensor_scalar(
+                out=sign_a[:], in0=gains[:, 0:1], scalar1=0.0, scalar2=2.0, op0=ALU.is_ge, op1=ALU.mult
+            )
+            nc.vector.tensor_scalar_add(sign_a[:], sign_a[:], -1.0)
+            nc.vector.tensor_tensor(out=squares[:], in0=gains[:], in1=gains[:], op=ALU.mult)
+            nc.vector.scalar_tensor_tensor(
+                out=norm2[:], in0=squares[:, 0:1], scalar=TINY, in1=squares[:, 1:2], op0=ALU.max, op1=ALU.add
+            )
+            nc.gpsimd.tensor_tensor(out=inv_norm[:], in0=norm2[:], in1=minus_half[:], op=ALU.pow)
+            nc.vector.tensor_tensor(out=inv_norm[:], in0=inv_norm[:], in1=sign_a[:], op=ALU.mult)
+            nc.vector.tensor_scalar_mul(cos_sin[:], gains[:], inv_norm[:, 0:1])
+            nc.vector.tensor_tensor(out=gain[:], in0=norm2[:], in1=inv_norm[:], op=ALU.mult)
+            nc.vector.tensor_copy(out=phase[:, 0:1], in_=cos_sin[:, 1:2])
+            nc.vector.tensor_scalar_add(phase[:, 1:2], cos_sin[:, 1:2], HALF_PI)
+
+        def newton_step():
+            nc.scalar.activation(out=sin_cos_now[:], in_=phase[:], func=ACT.Sin)
+            nc.vector.scalar_tensor_tensor(
+                out=step[:], in0=sin_cos_now[:, 0:1], scalar=cos_sin[:, 0:1], in1=phase[:, 0:1],
+                op0=ALU.mult, op1=ALU.subtract,
+            )
+            nc.vector.scalar_tensor_tensor(
+                out=phase[:, 0:1], in0=sin_cos_now[:, 1:2], scalar=cos_sin[:, 1:2], in1=step[:],
+                op0=ALU.mult, op1=ALU.subtract,
+            )
+            nc.vector.tensor_scalar_add(phase[:, 1:2], phase[:, 0:1], HALF_PI)
+
+        sums_of = {}
+        angle_of = {}
+        h2_of = {}
+        acc_of = {}
+
+        def first_product(r):
+            half, c = divmod(r, W2_CHUNKS)
+            for m in range(ROW_TILES * c, ROW_TILES * (c + 1)):
+                sums = sums_pool.tile([P, HALF], F32)
+                for k in range(PASSES):
+                    nc.tensor.matmul_mx(
+                        out=sums[:],
+                        lhsT=w2_codes[:, m, k, :].bitcast(FP8X4),
+                        lhsT_scale=w2_scales[:, m, k, :],
+                        rhs=h1_codes[:, half, k, :].bitcast(FP8X4),
+                        rhs_scale=h1_scales[:, half, k, :],
+                        start=(k == 0),
+                        stop=(k == PASSES - 1),
+                    )
+                sums_of[(half, m)] = sums
+
+        def take_off_turns(r):
+            half, c = divmod(r, W2_CHUNKS)
+            for m in range(ROW_TILES * c, ROW_TILES * (c + 1)):
+                group, place = divmod(m, PACK)
+                if place == 0:
+                    angle = angle_pool.tile([P, PACK, HALF], F32)
+                    angle_of[(half, group)] = angle
+                sums = sums_of[(half, m)]
+                turns = turns_pool.tile([P, HALF], I32)
+                nc.vector.tensor_scalar(
+                    out=turns[:], in0=sums[:], scalar1=1.0 / TWO_PI, scalar2=bias_turns[:, m : m + 1],
+                    op0=ALU.mult, op1=ALU.add,
+                )
+                nc.vector.scalar_tensor_tensor(
+                    out=angle_of[(half, group)][:, place, :], in0=turns[:], scalar=-TWO_PI, in1=sums[:],
+                    op0=ALU.mult, op1=ALU.add,
+                )
+
+        def sine(r):
+            half, c = divmod(r, W2_CHUNKS)
+            for m in range(ROW_TILES * c, ROW_TILES * (c + 1)):
+                group, place = divmod(m, PACK)
+                angle = angle_of[(half, group)]
+                nc.scalar.activation(
+                    out=angle[:, place, :], in_=angle[:, place, :], func=ACT.Sin, bias=bias[:, m : m + 1]
+                )
+
+        def scale_and_regroup(half, group):
+            h2 = h2_pool.tile([P, HALF, PACK], BF16, align_bytes=64)
+            sines = angle_of[(half, group)][:].rearrange("p t n -> p n t")
+            for part in range(TILES_PER_HALF):
+                cols = slice(part * P, (part + 1) * P)
+                if part % 2 == 0:
+                    nc.scalar.activation(
+                        out=h2[:, cols, :], in_=sines[:, cols, :], func=ACT.Copy, scale=gain[:, 0:1]
+                    )
+                else:
+                    nc.vector.tensor_scalar_mul(h2[:, cols, :], sines[:, cols, :], gain[:, 0:1])
+            h2_of[(half, group)] = h2
+
+        def quantise_h2(half, group):
+            for part in range(TILES_PER_HALF):
+                cols = slice(part * P, (part + 1) * P)
+                nc.vector.quantize_mx(
+                    out=h2_codes[:, half, group, cols].bitcast(FP8X4),
+                    scales=h2_scales[:, half, group, cols],
+                    in_=h2_of[(half, group)][:, cols, :].rearrange("p n t -> p (n t)"),
+                )
+
+        def second_product(half, group):
+            for part in range(TILES_PER_HALF):
+                cols = slice(part * P, (part + 1) * P)
+                if group == 0:
+                    acc = bank_pool.tile([P, D_MODEL], F32, tag="bank")
+                    acc_of[(half, part)] = acc
+                nc.tensor.matmul_mx(
+                    out=acc_of[(half, part)][:],
+                    lhsT=h2_codes[:, half, group, cols].bitcast(FP8X4),
+                    lhsT_scale=h2_scales[:, half, group, cols],
+                    rhs=w3_codes[:, group, :].bitcast(FP8X4),
+                    rhs_scale=w3_scales[:, group, :],
+                    start=(group == 0),
+                    stop=(group == PASSES - 1),
+                )
+
+        def finish(half):
+            for part in range(TILES_PER_HALF):
+                t = half * TILES_PER_HALF + part
+                nc.vector.tensor_tensor(
+                    out=residual[:, t, :], in0=acc_of[(half, part)][:], in1=residual[:, t, :], op=ALU.add
+                )
+                nc.sync.dma_start(out=out_rows[t * P : (t + 1) * P, :], in_=residual[:, t, :])
+
+        for i in range(RAW_BUFS):
+            load(i)
+        wave_constants()
+        for i in range(NEWTON_STEPS):
+            prepare_next()
+            newton_step()
+        nc.vector.tensor_scalar_add(bias[:], b2_bf[:], phase[:, 0:1])
+        nc.vector.tensor_scalar_mul(bias_turns[:], bias[:], 1.0 / TWO_PI)
+
+        rounds = HALVES * W2_CHUNKS
+        rounds_per_group = PACK // ROW_TILES
+        second_start = W2_CHUNKS + 2
+        for r in range(second_start + HALVES * PASSES + 1):
+            if r + 1 < W2_CHUNKS:
+                prepare_next()
+            elif r + 1 == W2_CHUNKS:
+                prepare_next()
+                prepare_next()
+            elif next_chunk[0] < len(chunks):
+                prepare_next()
+            if r - second_start in (PASSES, HALVES * PASSES):
+                finish((r - second_start) // PASSES - 1)
+            if r < rounds:
+                first_product(r)
+                take_off_turns(r)
+            if 0 <= r - 1 < rounds:
+                sine(r - 1)
+                if r % rounds_per_group == 0:
+                    scale_and_regroup(*divmod((r - 1) // rounds_per_group, PASSES))
+            if 0 <= r - 2 < rounds and (r - 1) % rounds_per_group == 0:
+                quantise_h2(*divmod((r - 2) // rounds_per_group, PASSES))
+            if 0 <= r - second_start < HALVES * PASSES:
+                second_product(*divmod(r - second_start, PASSES))

@@ -50,7 +50,7 @@ def tile_transreachencoderlayer_pb_kernel(
         keep = ctx.enter_context(tc.tile_pool(name="keep", bufs=1))
         raw_pool = ctx.enter_context(tc.tile_pool(name="raw", bufs=RAW_BUFS))
         grouped_pool = ctx.enter_context(tc.tile_pool(name="grouped", bufs=3))
-        turns_pool = ctx.enter_context(tc.tile_pool(name="turns", bufs=2))
+        turns_pool = ctx.enter_context(tc.tile_pool(name="turns", bufs=4))
         angle_pool = ctx.enter_context(tc.tile_pool(name="angle", bufs=3))
         h2_pool = ctx.enter_context(tc.tile_pool(name="h2", bufs=2))
         bank_pool = ctx.enter_context(tc.psum_pool(name="bank", bufs=4))
@@ -79,7 +79,9 @@ def tile_transreachencoderlayer_pb_kernel(
         residual = keep.tile([P, TOKEN_TILES, D_MODEL], F32)
         b3_rows = keep.tile([P, D_MODEL], BF16)
 
-        def load_chunk(i):
+        def load(i):
+            if i >= len(chunks):
+                return
             kind, c = chunks[i]
             rows = slice(c * CHUNK_ROWS, (c + 1) * CHUNK_ROWS)
             raw = raw_pool.tile([P, ROW_TILES, D_FF], BF16, tag="raw")
@@ -93,19 +95,13 @@ def tile_transreachencoderlayer_pb_kernel(
             raw_tiles[i] = raw
 
         def load_residual():
-            x1_raw = raw_pool.tile([P, TOKEN_TILES, D_MODEL], BF16, tag="raw")
+            x1_raw = grouped_pool.tile([P, TOKEN_TILES, D_MODEL], BF16, tag="grouped", align_bytes=64)
             nc.sync.dma_start(out=b3_rows[:], in_=ffn_b3.partition_broadcast(P))
             nc.sync.dma_start(out=x1_raw[:], in_=x1_rows.rearrange("(t p) d -> p t d", p=P))
             for t in range(TOKEN_TILES):
                 nc.gpsimd.tensor_tensor(
                     out=residual[:, t, :], in0=x1_raw[:, t, :], in1=b3_rows[:], op=ALU.add
                 )
-
-        def load(i):
-            if i < len(chunks):
-                load_chunk(i)
-            elif i == len(chunks):
-                load_residual()
 
         next_chunk = [0]
 
@@ -114,7 +110,7 @@ def tile_transreachencoderlayer_pb_kernel(
             next_chunk[0] = i + 1
             kind, c = chunks[i]
             words = raw_tiles[i][:].rearrange("p r k -> p (r k)").bitcast(F32)
-            grouped = grouped_pool.tile([P, ROW_TILES * D_FF], BF16, align_bytes=64)
+            grouped = grouped_pool.tile([P, ROW_TILES * D_FF], BF16, tag="grouped", align_bytes=64)
             grouped_words = grouped[:].bitcast(F32)
             if kind == "w2":
                 target = grouped_words.rearrange(
@@ -138,14 +134,15 @@ def tile_transreachencoderlayer_pb_kernel(
                         out=target[:, r, passes, :, :] if kind == "w2" else target[:, passes, r, :, :],
                         in_=bank[:].rearrange("q k u i -> q k i u"),
                     )
+                if kind == "w2":
+                    m = ROW_TILES * c + r
+                    nc.vector.quantize_mx(
+                        out=w2_codes[:, m, :, :].rearrange("p k o -> p (k o)").bitcast(FP8X4),
+                        scales=w2_scales[:, m, :, :].rearrange("p k o -> p (k o)"),
+                        in_=grouped[:, r * D_FF : (r + 1) * D_FF],
+                    )
             load(i + RAW_BUFS)
             if kind == "w2":
-                tiles = slice(ROW_TILES * c, ROW_TILES * (c + 1))
-                nc.vector.quantize_mx(
-                    out=w2_codes[:, tiles, :, :].rearrange("p m k o -> p (m k o)").bitcast(FP8X4),
-                    scales=w2_scales[:, tiles, :, :].rearrange("p m k o -> p (m k o)"),
-                    in_=grouped[:],
-                )
                 return
             for k in range(PASSES):
                 if kind == "h1":
@@ -239,20 +236,23 @@ def tile_transreachencoderlayer_pb_kernel(
 
         def take_off_turns(r):
             half, c = divmod(r, W2_CHUNKS)
-            for m in range(ROW_TILES * c, ROW_TILES * (c + 1)):
+            tiles = range(ROW_TILES * c, ROW_TILES * (c + 1))
+            turns_of = {}
+            for m in tiles:
+                turns = turns_pool.tile([P, HALF], I32)
+                nc.vector.tensor_scalar(
+                    out=turns[:], in0=sums_of[(half, m)][:], scalar1=1.0 / TWO_PI,
+                    scalar2=bias_turns[:, m : m + 1], op0=ALU.mult, op1=ALU.add,
+                )
+                turns_of[m] = turns
+            for m in tiles:
                 group, place = divmod(m, PACK)
                 if place == 0:
                     angle = angle_pool.tile([P, PACK, HALF], F32)
                     angle_of[(half, group)] = angle
-                sums = sums_of[(half, m)]
-                turns = turns_pool.tile([P, HALF], I32)
-                nc.vector.tensor_scalar(
-                    out=turns[:], in0=sums[:], scalar1=1.0 / TWO_PI, scalar2=bias_turns[:, m : m + 1],
-                    op0=ALU.mult, op1=ALU.add,
-                )
                 nc.vector.scalar_tensor_tensor(
-                    out=angle_of[(half, group)][:, place, :], in0=turns[:], scalar=-TWO_PI, in1=sums[:],
-                    op0=ALU.mult, op1=ALU.add,
+                    out=angle_of[(half, group)][:, place, :], in0=turns_of[m][:], scalar=-TWO_PI,
+                    in1=sums_of[(half, m)][:], op0=ALU.mult, op1=ALU.add,
                 )
 
         def sine(r):
@@ -330,6 +330,8 @@ def tile_transreachencoderlayer_pb_kernel(
                 prepare_next()
             elif next_chunk[0] < len(chunks):
                 prepare_next()
+                if next_chunk[0] == len(chunks):
+                    load_residual()
             if r - second_start in (PASSES, HALVES * PASSES):
                 finish((r - second_start) // PASSES - 1)
             if r < rounds:

@@ -55,7 +55,6 @@ def tile_transreachencoderlayer_pb_kernel(
         h2_pool = ctx.enter_context(tc.tile_pool(name="h2", bufs=2))
         bank_pool = ctx.enter_context(tc.psum_pool(name="bank", bufs=4))
         sums_pool = ctx.enter_context(tc.psum_pool(name="sums", bufs=4))
-        ctx.enter_context(tc.manual_schedule())
 
         h1_codes = keep.tile([P, HALVES, PASSES, HALF], U32, align_bytes=64)
         h1_scales = keep.tile([P, HALVES, PASSES, HALF], U8, align_bytes=64)

@@ -30,7 +30,9 @@ W2_CHUNKS = D_FF // CHUNK_ROWS
 TOKEN_TILES = TOKENS // P
 TILES_PER_HALF = HALF // P
 RAW_BUFS = 6
+FIRST_CHUNKS = 3
 NEWTON_STEPS = 3
+RUN = 4
 TWO_PI = 2.0 * math.pi
 HALF_PI = 0.5 * math.pi
 TINY = 1e-36
@@ -55,6 +57,7 @@ def tile_transreachencoderlayer_pb_kernel(
         h2_pool = ctx.enter_context(tc.tile_pool(name="h2", bufs=2))
         bank_pool = ctx.enter_context(tc.psum_pool(name="bank", bufs=4))
         sums_pool = ctx.enter_context(tc.psum_pool(name="sums", bufs=4))
+        ctx.enter_context(tc.manual_schedule())
 
         h1_codes = keep.tile([P, HALVES, PASSES, HALF], U32, align_bytes=64)
         h1_scales = keep.tile([P, HALVES, PASSES, HALF], U8, align_bytes=64)
@@ -177,10 +180,6 @@ def tile_transreachencoderlayer_pb_kernel(
         def wave_constants():
             nc.scalar.dma_start(out=a_bf[:], in_=ffn_a2w1.partition_broadcast(P))
             nc.scalar.dma_start(out=b_bf[:], in_=ffn_a2w2.partition_broadcast(P))
-            nc.scalar.dma_start(
-                out=b2_bf[:].rearrange("p (c e) -> p c e", e=2),
-                in_=ffn_b2.rearrange("(c p e) -> p c e", p=P, e=2),
-            )
             nc.vector.memset(minus_half[:], -0.5)
             nc.scalar.activation(out=step[:], in_=minus_half[:], func=ACT.Sin)
             nc.vector.tensor_copy(out=gains[:, 0:1], in_=a_bf[:])
@@ -247,7 +246,7 @@ def tile_transreachencoderlayer_pb_kernel(
             for m in tiles:
                 group, place = divmod(m, PACK)
                 if place == 0:
-                    angle = angle_pool.tile([P, PACK, HALF], F32)
+                    angle = angle_pool.tile([P, PACK, HALF], F32, tag="angle")
                     angle_of[(half, group)] = angle
                 nc.vector.scalar_tensor_tensor(
                     out=angle_of[(half, group)][:, place, :], in0=turns_of[m][:], scalar=-TWO_PI,
@@ -265,15 +264,16 @@ def tile_transreachencoderlayer_pb_kernel(
 
         def scale_and_regroup(half, group):
             h2 = h2_pool.tile([P, HALF, PACK], BF16, align_bytes=64)
-            sines = angle_of[(half, group)][:].rearrange("p t n -> p n t")
+            sines = angle_of[(half, group)][:].rearrange("p t (c i) -> p c t i", i=RUN)
+            words = h2[:].rearrange("p (c i) t -> p c t i", i=RUN)
             for part in range(TILES_PER_HALF):
-                cols = slice(part * P, (part + 1) * P)
+                runs = slice(part * P // RUN, (part + 1) * P // RUN)
                 if part % 2 == 0:
                     nc.scalar.activation(
-                        out=h2[:, cols, :], in_=sines[:, cols, :], func=ACT.Copy, scale=gain[:, 0:1]
+                        out=words[:, runs, :, :], in_=sines[:, runs, :, :], func=ACT.Copy, scale=gain[:, 0:1]
                     )
                 else:
-                    nc.vector.tensor_scalar_mul(h2[:, cols, :], sines[:, cols, :], gain[:, 0:1])
+                    nc.vector.tensor_scalar_mul(words[:, runs, :, :], sines[:, runs, :, :], gain[:, 0:1])
             h2_of[(half, group)] = h2
 
         def quantise_h2(half, group):
@@ -302,17 +302,31 @@ def tile_transreachencoderlayer_pb_kernel(
                 )
 
         def finish(half):
+            if half == 0:
+                product = angle_pool.tile([P, TILES_PER_HALF, D_MODEL], F32, tag="angle")
             for part in range(TILES_PER_HALF):
                 t = half * TILES_PER_HALF + part
-                nc.vector.tensor_tensor(
-                    out=residual[:, t, :], in0=acc_of[(half, part)][:], in1=residual[:, t, :], op=ALU.add
-                )
+                if half == 0:
+                    nc.scalar.copy(out=product[:, part, :], in_=acc_of[(half, part)][:])
+                    nc.gpsimd.tensor_tensor(
+                        out=residual[:, t, :], in0=product[:, part, :], in1=residual[:, t, :], op=ALU.add
+                    )
+                else:
+                    nc.vector.tensor_tensor(
+                        out=residual[:, t, :], in0=acc_of[(half, part)][:], in1=residual[:, t, :], op=ALU.add
+                    )
                 nc.sync.dma_start(out=out_rows[t * P : (t + 1) * P, :], in_=residual[:, t, :])
 
         for i in range(RAW_BUFS):
             load(i)
+            if i + 1 == FIRST_CHUNKS:
+                nc.sync.dma_start(
+                    out=b2_bf[:].rearrange("p (c e) -> p c e", e=2),
+                    in_=ffn_b2.rearrange("(c p e) -> p c e", p=P, e=2),
+                )
         wave_constants()
-        for i in range(NEWTON_STEPS):
+        assert NEWTON_STEPS == FIRST_CHUNKS
+        for i in range(FIRST_CHUNKS):
             prepare_next()
             newton_step()
         nc.vector.tensor_scalar_add(bias[:], b2_bf[:], phase[:, 0:1])
@@ -320,7 +334,7 @@ def tile_transreachencoderlayer_pb_kernel(
 
         rounds = HALVES * W2_CHUNKS
         rounds_per_group = PACK // ROW_TILES
-        second_start = W2_CHUNKS + 2
+        second_start = W2_CHUNKS + 3
         for r in range(second_start + HALVES * PASSES + 1):
             if r + 1 < W2_CHUNKS:
                 prepare_next()
@@ -338,9 +352,9 @@ def tile_transreachencoderlayer_pb_kernel(
                 take_off_turns(r)
             if 0 <= r - 1 < rounds:
                 sine(r - 1)
-                if r % rounds_per_group == 0:
-                    scale_and_regroup(*divmod((r - 1) // rounds_per_group, PASSES))
             if 0 <= r - 2 < rounds and (r - 1) % rounds_per_group == 0:
-                quantise_h2(*divmod((r - 2) // rounds_per_group, PASSES))
+                scale_and_regroup(*divmod((r - 2) // rounds_per_group, PASSES))
+            if 0 <= r - 3 < rounds and r % rounds_per_group == 0:
+                quantise_h2(*divmod((r - 3) // rounds_per_group, PASSES))
             if 0 <= r - second_start < HALVES * PASSES:
                 second_product(*divmod(r - second_start, PASSES))

@@ -30,7 +30,11 @@ W2_CHUNKS = D_FF // CHUNK_ROWS
 TOKEN_TILES = TOKENS // P
 TILES_PER_HALF = HALF // P
 RAW_BUFS = 6
-FIRST_CHUNKS = 3
+SPLIT_LOADS = 4
+VECTOR_COPIES = 2
+QUARTER = 256
+BLOCKS = ((0, HALF), (HALF, QUARTER), (HALF + QUARTER, QUARTER))
+BLOCK_BUFS = {HALF: (3, 2), QUARTER: (4, 3)}
 NEWTON_STEPS = 3
 RUN = 4
 TWO_PI = 2.0 * math.pi
@@ -65,20 +69,20 @@ def tile_transreachencoderlayer_pb_kernel(
         w2_scales = keep.tile([P, FEATURE_TILES, PASSES, P], U8, align_bytes=64)
         w3_codes = keep.tile([P, PASSES, D_MODEL], U32, align_bytes=64)
         w3_scales = keep.tile([P, PASSES, D_MODEL], U8, align_bytes=64)
-        h2_codes = keep.tile([P, HALVES, PASSES, HALF], U32, align_bytes=64)
-        h2_scales = keep.tile([P, HALVES, PASSES, HALF], U8, align_bytes=64)
+        h2_codes = keep.tile([P, PASSES, TOKENS], U32, align_bytes=64)
+        h2_scales = keep.tile([P, PASSES, TOKENS], U8, align_bytes=64)
 
         identity = keep.tile([P, P], F32)
         make_identity(nc, identity[:])
 
         chunks = (
-            [("h1", c) for c in range(2)]
-            + [("w2", c) for c in range(W2_CHUNKS)]
-            + [("h1", c) for c in range(2, 4)]
-            + [("w3", c) for c in range(2)]
+            [("h1", 0), ("w2", 0), ("h1", 1)]
+            + [("w2", c) for c in range(1, 6)]
+            + [("h1", 2), ("w2", 6), ("w2", 7), ("h1", 3), ("w3", 0), ("w3", 1)]
         )
+        position = {chunk: i for i, chunk in enumerate(chunks)}
         raw_tiles = {}
-        residual = keep.tile([P, TOKEN_TILES, D_MODEL], F32)
+        residual = {}
         b3_rows = keep.tile([P, D_MODEL], BF16)
 
         def load(i):
@@ -93,72 +97,112 @@ def tile_transreachencoderlayer_pb_kernel(
                 source = ffn_w3[rows, :].rearrange("(r p) k -> p r k", p=P)
             else:
                 source = ffn_w2[rows, :].rearrange("(p r) k -> p r k", p=P)
-            nc.sync.dma_start(out=raw[:], in_=source)
+            if i < SPLIT_LOADS and kind == "h1":
+                for j in range(2):
+                    cols = slice(j * D_FF // 2, (j + 1) * D_FF // 2)
+                    nc.sync.dma_start(out=raw[:, :, cols], in_=source[:, :, cols])
+            elif i < SPLIT_LOADS:
+                for r in range(ROW_TILES):
+                    nc.sync.dma_start(out=raw[:, r, :], in_=source[:, r, :])
+            else:
+                nc.sync.dma_start(out=raw[:], in_=source)
             raw_tiles[i] = raw
 
+        x1_raw_of = []
+
+        def residual_of(t):
+            half, part = divmod(t, TILES_PER_HALF)
+            return residual[half][:, part, :]
+
         def load_residual():
-            x1_raw = grouped_pool.tile([P, TOKEN_TILES, D_MODEL], BF16, tag="grouped", align_bytes=64)
+            x1_raw = raw_pool.tile([P, TOKEN_TILES, D_MODEL], BF16, tag="raw")
+            for half in range(HALVES):
+                residual_tile = raw_pool.tile([P, TILES_PER_HALF, D_MODEL], F32, tag="raw")
+                residual[half] = residual_tile
             nc.sync.dma_start(out=b3_rows[:], in_=ffn_b3.partition_broadcast(P))
             nc.sync.dma_start(out=x1_raw[:], in_=x1_rows.rearrange("(t p) d -> p t d", p=P))
-            for t in range(TOKEN_TILES):
+            x1_raw_of.append(x1_raw)
+
+        def add_b3(t):
+            x1_raw = x1_raw_of[0]
+            for d in range(0, D_MODEL, P):
+                cols = slice(d, d + P)
                 nc.gpsimd.tensor_tensor(
-                    out=residual[:, t, :], in0=x1_raw[:, t, :], in1=b3_rows[:], op=ALU.add
+                    out=residual_of(t)[:, cols], in0=x1_raw[:, t, cols], in1=b3_rows[:, cols], op=ALU.add
                 )
 
-        next_chunk = [0]
+        grouped_of = {}
 
-        def prepare_next():
-            i = next_chunk[0]
-            next_chunk[0] = i + 1
+        def transpose_bank(i, r, j):
             kind, c = chunks[i]
             words = raw_tiles[i][:].rearrange("p r k -> p (r k)").bitcast(F32)
-            grouped = grouped_pool.tile([P, ROW_TILES * D_FF], BF16, tag="grouped", align_bytes=64)
-            grouped_words = grouped[:].bitcast(F32)
+            if i not in grouped_of:
+                grouped_tile = grouped_pool.tile([P, ROW_TILES * D_FF], BF16, tag="grouped", align_bytes=64)
+                grouped_of[i] = grouped_tile
+            grouped_words = grouped_of[i][:].bitcast(F32)
             if kind == "w2":
                 target = grouped_words.rearrange(
-                    "p (r k i u) -> p r k i u", r=ROW_TILES, k=PASSES, i=P
+                    "p (r k i u) -> p k r i u", r=ROW_TILES, k=PASSES, i=P
                 )
             else:
                 target = grouped_words.rearrange(
                     "p (k r i u) -> p k r i u", r=ROW_TILES, k=PASSES, i=P
                 )
+            bank = bank_pool.tile([P, 2, 2, P], F32, tag="bank")
+            for k in range(2):
+                for u in range(2):
+                    first = r * WORDS + ((2 * j + k) * 2 + u) * P
+                    nc.tensor.transpose(bank[:, k, u, :], words[:, first : first + P], identity[:])
+            copy = nc.vector.tensor_copy if i < VECTOR_COPIES and (r + j) % 2 else nc.scalar.copy
+            copy(
+                out=target[:, 2 * j : 2 * j + 2, r, :, :], in_=bank[:].rearrange("q k u i -> q k i u")
+            )
+
+        def quantise_w2(m):
+            c, r = divmod(m, ROW_TILES)
+            nc.vector.quantize_mx(
+                out=w2_codes[:, m, :, :].rearrange("p k o -> p (k o)").bitcast(FP8X4),
+                scales=w2_scales[:, m, :, :].rearrange("p k o -> p (k o)"),
+                in_=grouped_of[position[("w2", c)]][:, r * D_FF : (r + 1) * D_FF],
+            )
+
+        def quantise_moving(kind, c, k):
+            grouped = grouped_of[position[(kind, c)]]
+            if kind == "h1":
+                half, part = divmod(c, HALF // CHUNK_ROWS)
+                cols = slice(part * CHUNK_ROWS, (part + 1) * CHUNK_ROWS)
+                codes, scales = h1_codes[:, half, k, cols], h1_scales[:, half, k, cols]
+            else:
+                cols = slice(c * CHUNK_ROWS, (c + 1) * CHUNK_ROWS)
+                codes, scales = w3_codes[:, k, cols], w3_scales[:, k, cols]
+            nc.vector.quantize_mx(
+                out=codes.bitcast(FP8X4),
+                scales=scales,
+                in_=grouped[:, k * CHUNK_ROWS * PACK : (k + 1) * CHUNK_ROWS * PACK],
+            )
+
+        def quantise_half(kind, c, j):
+            quantise_moving(kind, c, 2 * j)
+            quantise_moving(kind, c, 2 * j + 1)
+
+        def transpose_w2(c):
+            i = position[("w2", c)]
             for r in range(ROW_TILES):
-                for j in range(PASSES // 2):
-                    bank = bank_pool.tile([P, 2, 2, P], F32, tag="bank")
-                    for k in range(2):
-                        for u in range(2):
-                            first = r * WORDS + ((2 * j + k) * 2 + u) * P
-                            nc.tensor.transpose(
-                                bank[:, k, u, :], words[:, first : first + P], identity[:]
-                            )
-                    passes = slice(2 * j, 2 * j + 2)
-                    nc.scalar.copy(
-                        out=target[:, r, passes, :, :] if kind == "w2" else target[:, passes, r, :, :],
-                        in_=bank[:].rearrange("q k u i -> q k i u"),
-                    )
-                if kind == "w2":
-                    m = ROW_TILES * c + r
-                    nc.vector.quantize_mx(
-                        out=w2_codes[:, m, :, :].rearrange("p k o -> p (k o)").bitcast(FP8X4),
-                        scales=w2_scales[:, m, :, :].rearrange("p k o -> p (k o)"),
-                        in_=grouped[:, r * D_FF : (r + 1) * D_FF],
-                    )
+                for j in range(2):
+                    transpose_bank(i, r, j)
             load(i + RAW_BUFS)
-            if kind == "w2":
-                return
-            for k in range(PASSES):
-                if kind == "h1":
-                    half, part = divmod(c, HALF // CHUNK_ROWS)
-                    cols = slice(part * CHUNK_ROWS, (part + 1) * CHUNK_ROWS)
-                    codes, scales = h1_codes[:, half, k, cols], h1_scales[:, half, k, cols]
-                else:
-                    cols = slice(c * CHUNK_ROWS, (c + 1) * CHUNK_ROWS)
-                    codes, scales = w3_codes[:, k, cols], w3_scales[:, k, cols]
-                nc.vector.quantize_mx(
-                    out=codes.bitcast(FP8X4),
-                    scales=scales,
-                    in_=grouped[:, k * CHUNK_ROWS * PACK : (k + 1) * CHUNK_ROWS * PACK],
-                )
+
+        def transpose_half(kind, c, j):
+            i = position[(kind, c)]
+            for r in range(ROW_TILES):
+                transpose_bank(i, r, j)
+            if j == 1:
+                load(i + RAW_BUFS)
+
+        def prepare_h1(c):
+            for j in range(2):
+                transpose_half("h1", c, j)
+                quantise_half("h1", c, j)
 
         a_bf = keep.tile([P, 1], BF16)
         b_bf = keep.tile([P, 1], BF16)
@@ -173,6 +217,7 @@ def tile_transreachencoderlayer_pb_kernel(
         gain = keep.tile([P, 1], F32)
         phase = keep.tile([P, 2], F32)
         sin_cos_now = keep.tile([P, 2], F32)
+        terms = keep.tile([P, 2], F32)
         step = keep.tile([P, 1], F32)
         bias = keep.tile([P, FEATURE_TILES], F32)
         bias_turns = keep.tile([P, FEATURE_TILES], F32)
@@ -180,181 +225,285 @@ def tile_transreachencoderlayer_pb_kernel(
         def wave_constants():
             nc.scalar.dma_start(out=a_bf[:], in_=ffn_a2w1.partition_broadcast(P))
             nc.scalar.dma_start(out=b_bf[:], in_=ffn_a2w2.partition_broadcast(P))
-            nc.vector.memset(minus_half[:], -0.5)
+            nc.gpsimd.memset(minus_half[:], -0.5)
             nc.scalar.activation(out=step[:], in_=minus_half[:], func=ACT.Sin)
-            nc.vector.tensor_copy(out=gains[:, 0:1], in_=a_bf[:])
-            nc.vector.tensor_copy(out=gains[:, 1:2], in_=b_bf[:])
-            nc.vector.tensor_scalar(
+            nc.gpsimd.tensor_copy(out=gains[:, 0:1], in_=a_bf[:])
+            nc.gpsimd.tensor_copy(out=gains[:, 1:2], in_=b_bf[:])
+            nc.gpsimd.tensor_scalar(
                 out=sign_a[:], in0=gains[:, 0:1], scalar1=0.0, scalar2=2.0, op0=ALU.is_ge, op1=ALU.mult
             )
-            nc.vector.tensor_scalar_add(sign_a[:], sign_a[:], -1.0)
-            nc.vector.tensor_tensor(out=squares[:], in0=gains[:], in1=gains[:], op=ALU.mult)
-            nc.vector.scalar_tensor_tensor(
-                out=norm2[:], in0=squares[:, 0:1], scalar=TINY, in1=squares[:, 1:2], op0=ALU.max, op1=ALU.add
+            nc.gpsimd.tensor_scalar(
+                out=sign_a[:], in0=sign_a[:], scalar1=1.0, scalar2=-1.0, op0=ALU.mult, op1=ALU.add
+            )
+            nc.gpsimd.tensor_tensor(out=squares[:], in0=gains[:], in1=gains[:], op=ALU.mult)
+            nc.gpsimd.tensor_scalar(
+                out=norm2[:], in0=squares[:, 0:1], scalar1=TINY, scalar2=squares[:, 1:2],
+                op0=ALU.max, op1=ALU.add,
             )
             nc.gpsimd.tensor_tensor(out=inv_norm[:], in0=norm2[:], in1=minus_half[:], op=ALU.pow)
-            nc.vector.tensor_tensor(out=inv_norm[:], in0=inv_norm[:], in1=sign_a[:], op=ALU.mult)
-            nc.vector.tensor_scalar_mul(cos_sin[:], gains[:], inv_norm[:, 0:1])
-            nc.vector.tensor_tensor(out=gain[:], in0=norm2[:], in1=inv_norm[:], op=ALU.mult)
-            nc.vector.tensor_copy(out=phase[:, 0:1], in_=cos_sin[:, 1:2])
-            nc.vector.tensor_scalar_add(phase[:, 1:2], cos_sin[:, 1:2], HALF_PI)
+            nc.gpsimd.tensor_tensor(out=inv_norm[:], in0=inv_norm[:], in1=sign_a[:], op=ALU.mult)
+            nc.gpsimd.tensor_scalar(
+                out=cos_sin[:], in0=gains[:], scalar1=inv_norm[:, 0:1], scalar2=0.0, op0=ALU.mult, op1=ALU.add
+            )
+            nc.gpsimd.tensor_tensor(out=gain[:], in0=norm2[:], in1=inv_norm[:], op=ALU.mult)
+            nc.gpsimd.tensor_copy(out=phase[:, 0:1], in_=cos_sin[:, 1:2])
+            nc.gpsimd.tensor_scalar(
+                out=phase[:, 1:2], in0=cos_sin[:, 1:2], scalar1=1.0, scalar2=HALF_PI, op0=ALU.mult, op1=ALU.add
+            )
 
         def newton_step():
             nc.scalar.activation(out=sin_cos_now[:], in_=phase[:], func=ACT.Sin)
-            nc.vector.scalar_tensor_tensor(
-                out=step[:], in0=sin_cos_now[:, 0:1], scalar=cos_sin[:, 0:1], in1=phase[:, 0:1],
-                op0=ALU.mult, op1=ALU.subtract,
+            nc.gpsimd.tensor_tensor(out=terms[:], in0=sin_cos_now[:], in1=cos_sin[:], op=ALU.mult)
+            nc.gpsimd.tensor_tensor(out=step[:], in0=terms[:, 0:1], in1=terms[:, 1:2], op=ALU.subtract)
+            nc.gpsimd.tensor_scalar(
+                out=phase[:], in0=phase[:], scalar1=step[:, 0:1], scalar2=0.0, op0=ALU.subtract, op1=ALU.add
             )
-            nc.vector.scalar_tensor_tensor(
-                out=phase[:, 0:1], in0=sin_cos_now[:, 1:2], scalar=cos_sin[:, 1:2], in1=step[:],
-                op0=ALU.mult, op1=ALU.subtract,
+
+        def biases():
+            nc.gpsimd.tensor_scalar(
+                out=bias[:], in0=b2_bf[:], scalar1=phase[:, 0:1], scalar2=0.0, op0=ALU.add, op1=ALU.add
             )
-            nc.vector.tensor_scalar_add(phase[:, 1:2], phase[:, 0:1], HALF_PI)
+            nc.gpsimd.tensor_scalar(
+                out=bias_turns[:], in0=bias[:], scalar1=1.0 / TWO_PI, scalar2=0.0, op0=ALU.mult, op1=ALU.add
+            )
 
         sums_of = {}
+        turns_of = {}
         angle_of = {}
         h2_of = {}
         acc_of = {}
 
-        def first_product(r):
-            half, c = divmod(r, W2_CHUNKS)
-            for m in range(ROW_TILES * c, ROW_TILES * (c + 1)):
-                sums = sums_pool.tile([P, HALF], F32)
-                for k in range(PASSES):
-                    nc.tensor.matmul_mx(
-                        out=sums[:],
-                        lhsT=w2_codes[:, m, k, :].bitcast(FP8X4),
-                        lhsT_scale=w2_scales[:, m, k, :],
-                        rhs=h1_codes[:, half, k, :].bitcast(FP8X4),
-                        rhs_scale=h1_scales[:, half, k, :],
-                        start=(k == 0),
-                        stop=(k == PASSES - 1),
-                    )
-                sums_of[(half, m)] = sums
-
-        def take_off_turns(r):
-            half, c = divmod(r, W2_CHUNKS)
-            tiles = range(ROW_TILES * c, ROW_TILES * (c + 1))
-            turns_of = {}
-            for m in tiles:
-                turns = turns_pool.tile([P, HALF], I32)
-                nc.vector.tensor_scalar(
-                    out=turns[:], in0=sums_of[(half, m)][:], scalar1=1.0 / TWO_PI,
-                    scalar2=bias_turns[:, m : m + 1], op0=ALU.mult, op1=ALU.add,
-                )
-                turns_of[m] = turns
-            for m in tiles:
-                group, place = divmod(m, PACK)
-                if place == 0:
-                    angle = angle_pool.tile([P, PACK, HALF], F32, tag="angle")
-                    angle_of[(half, group)] = angle
-                nc.vector.scalar_tensor_tensor(
-                    out=angle_of[(half, group)][:, place, :], in0=turns_of[m][:], scalar=-TWO_PI,
-                    in1=sums_of[(half, m)][:], op0=ALU.mult, op1=ALU.add,
-                )
-
-        def sine(r):
-            half, c = divmod(r, W2_CHUNKS)
-            for m in range(ROW_TILES * c, ROW_TILES * (c + 1)):
-                group, place = divmod(m, PACK)
-                angle = angle_of[(half, group)]
-                nc.scalar.activation(
-                    out=angle[:, place, :], in_=angle[:, place, :], func=ACT.Sin, bias=bias[:, m : m + 1]
-                )
-
-        def scale_and_regroup(half, group):
-            h2 = h2_pool.tile([P, HALF, PACK], BF16, align_bytes=64)
-            sines = angle_of[(half, group)][:].rearrange("p t (c i) -> p c t i", i=RUN)
-            words = h2[:].rearrange("p (c i) t -> p c t i", i=RUN)
-            for part in range(TILES_PER_HALF):
-                runs = slice(part * P // RUN, (part + 1) * P // RUN)
-                if part % 2 == 0:
-                    nc.scalar.activation(
-                        out=words[:, runs, :, :], in_=sines[:, runs, :, :], func=ACT.Copy, scale=gain[:, 0:1]
-                    )
-                else:
-                    nc.vector.tensor_scalar_mul(words[:, runs, :, :], sines[:, runs, :, :], gain[:, 0:1])
-            h2_of[(half, group)] = h2
-
-        def quantise_h2(half, group):
-            for part in range(TILES_PER_HALF):
-                cols = slice(part * P, (part + 1) * P)
-                nc.vector.quantize_mx(
-                    out=h2_codes[:, half, group, cols].bitcast(FP8X4),
-                    scales=h2_scales[:, half, group, cols],
-                    in_=h2_of[(half, group)][:, cols, :].rearrange("p n t -> p (n t)"),
-                )
-
-        def second_product(half, group):
-            for part in range(TILES_PER_HALF):
-                cols = slice(part * P, (part + 1) * P)
-                if group == 0:
-                    acc = bank_pool.tile([P, D_MODEL], F32, tag="bank")
-                    acc_of[(half, part)] = acc
+        def first_product(block, m, cols=None):
+            first, width = BLOCKS[block]
+            per_bank = HALF // width
+            key = (block, m // per_bank)
+            if key not in sums_of:
+                sums_tile = sums_pool.tile([P, HALF], F32, tag="sums")
+                sums_of[key] = sums_tile
+            base = (m % per_bank) * width
+            lo, hi = cols or (0, width)
+            half, start_col = divmod(first, HALF)
+            for k in range(PASSES):
                 nc.tensor.matmul_mx(
-                    out=acc_of[(half, part)][:],
-                    lhsT=h2_codes[:, half, group, cols].bitcast(FP8X4),
-                    lhsT_scale=h2_scales[:, half, group, cols],
-                    rhs=w3_codes[:, group, :].bitcast(FP8X4),
-                    rhs_scale=w3_scales[:, group, :],
-                    start=(group == 0),
-                    stop=(group == PASSES - 1),
+                    out=sums_of[key][:, base + lo : base + hi],
+                    lhsT=w2_codes[:, m, k, :].bitcast(FP8X4),
+                    lhsT_scale=w2_scales[:, m, k, :],
+                    rhs=h1_codes[:, half, k, start_col + lo : start_col + hi].bitcast(FP8X4),
+                    rhs_scale=h1_scales[:, half, k, start_col + lo : start_col + hi],
+                    start=(k == 0),
+                    stop=(k == PASSES - 1),
                 )
 
-        def finish(half):
-            if half == 0:
-                product = angle_pool.tile([P, TILES_PER_HALF, D_MODEL], F32, tag="angle")
-            for part in range(TILES_PER_HALF):
-                t = half * TILES_PER_HALF + part
-                if half == 0:
-                    nc.scalar.copy(out=product[:, part, :], in_=acc_of[(half, part)][:])
-                    nc.gpsimd.tensor_tensor(
-                        out=residual[:, t, :], in0=product[:, part, :], in1=residual[:, t, :], op=ALU.add
-                    )
-                else:
-                    nc.vector.tensor_tensor(
-                        out=residual[:, t, :], in0=acc_of[(half, part)][:], in1=residual[:, t, :], op=ALU.add
-                    )
-                nc.sync.dma_start(out=out_rows[t * P : (t + 1) * P, :], in_=residual[:, t, :])
+        def count_turns(block, m):
+            first, width = BLOCKS[block]
+            per_bank = HALF // width
+            key = (block, m // per_bank)
+            if key not in turns_of:
+                turns_tile = turns_pool.tile([P, HALF], I32, tag="turns")
+                turns_of[key] = turns_tile
+            cols = slice((m % per_bank) * width, (m % per_bank + 1) * width)
+            nc.vector.tensor_scalar(
+                out=turns_of[key][:, cols], in0=sums_of[key][:, cols], scalar1=1.0 / TWO_PI,
+                scalar2=bias_turns[:, m : m + 1], op0=ALU.mult, op1=ALU.add,
+            )
+
+        def take_off_turns(block, b):
+            first, width = BLOCKS[block]
+            per_bank = HALF // width
+            group, place = divmod(b * per_bank, PACK)
+            if (block, group) not in angle_of:
+                angle_tile = angle_pool.tile([P, PACK, width], F32, tag="angle%d" % width, bufs=BLOCK_BUFS[width][0])
+                angle_of[(block, group)] = angle_tile
+            nc.vector.scalar_tensor_tensor(
+                out=angle_of[(block, group)][:, place : place + per_bank, :].rearrange("p t n -> p (t n)"),
+                in0=turns_of[(block, b)][:], scalar=-TWO_PI,
+                in1=sums_of[(block, b)][:], op0=ALU.mult, op1=ALU.add,
+            )
+
+        def sine(block, m):
+            group, place = divmod(m, PACK)
+            angle = angle_of[(block, group)]
+            nc.scalar.activation(
+                out=angle[:, place, :], in_=angle[:, place, :], func=ACT.Sin, bias=bias[:, m : m + 1]
+            )
+
+        def regroup(block, group, part, engine):
+            first, width = BLOCKS[block]
+            if (block, group) not in h2_of:
+                h2_tile = h2_pool.tile([P, width, PACK], BF16, tag="h2%d" % width, bufs=BLOCK_BUFS[width][1], align_bytes=64)
+                h2_of[(block, group)] = h2_tile
+            sines = angle_of[(block, group)][:].rearrange("p t (c i) -> p c t i", i=RUN)
+            words = h2_of[(block, group)][:].rearrange("p (c i) t -> p c t i", i=RUN)
+            runs = slice(part * P // RUN, (part + 1) * P // RUN)
+            if engine == "S":
+                nc.scalar.activation(
+                    out=words[:, runs, :, :], in_=sines[:, runs, :, :], func=ACT.Copy, scale=gain[:, 0:1]
+                )
+            elif engine == "V":
+                nc.vector.tensor_scalar_mul(words[:, runs, :, :], sines[:, runs, :, :], gain[:, 0:1])
+            else:
+                nc.gpsimd.tensor_scalar(
+                    out=words[:, runs, :, :], in0=sines[:, runs, :, :], scalar1=gain[:, 0:1], scalar2=0.0,
+                    op0=ALU.mult, op1=ALU.add,
+                )
+
+        def quantise_h2(block, group):
+            first, width = BLOCKS[block]
+            nc.vector.quantize_mx(
+                out=h2_codes[:, group, first : first + width].bitcast(FP8X4),
+                scales=h2_scales[:, group, first : first + width],
+                in_=h2_of[(block, group)][:].rearrange("p n t -> p (n t)"),
+            )
+
+        def second_product(t, group):
+            cols = slice(t * P, (t + 1) * P)
+            if group == 0:
+                acc_tile = bank_pool.tile([P, D_MODEL], F32, tag="bank")
+                acc_of[t] = acc_tile
+            nc.tensor.matmul_mx(
+                out=acc_of[t][:],
+                lhsT=h2_codes[:, group, cols].bitcast(FP8X4),
+                lhsT_scale=h2_scales[:, group, cols],
+                rhs=w3_codes[:, group, :].bitcast(FP8X4),
+                rhs_scale=w3_scales[:, group, :],
+                start=(group == 0),
+                stop=(group == PASSES - 1),
+            )
+
+        def finish(t):
+            nc.vector.tensor_tensor(
+                out=residual_of(t), in0=acc_of[t][:], in1=residual_of(t), op=ALU.add
+            )
+            nc.sync.dma_start(out=out_rows[t * P : (t + 1) * P, :], in_=residual_of(t))
 
         for i in range(RAW_BUFS):
             load(i)
-            if i + 1 == FIRST_CHUNKS:
+            if i == 2:
                 nc.sync.dma_start(
                     out=b2_bf[:].rearrange("p (c e) -> p c e", e=2),
                     in_=ffn_b2.rearrange("(c p e) -> p c e", p=P, e=2),
                 )
         wave_constants()
-        assert NEWTON_STEPS == FIRST_CHUNKS
-        for i in range(FIRST_CHUNKS):
-            prepare_next()
-            newton_step()
-        nc.vector.tensor_scalar_add(bias[:], b2_bf[:], phase[:, 0:1])
-        nc.vector.tensor_scalar_mul(bias_turns[:], bias[:], 1.0 / TWO_PI)
+        first_quarter, second_quarter = (0, QUARTER), (QUARTER, HALF)
+        prepare_h1(0)
+        newton_step()
+        transpose_w2(0)
+        quantise_w2(0)
+        quantise_w2(1)
+        newton_step()
+        for m in range(ROW_TILES):
+            first_product(0, m, first_quarter)
+        prepare_h1(1)
+        newton_step()
+        biases()
 
-        rounds = HALVES * W2_CHUNKS
-        rounds_per_group = PACK // ROW_TILES
-        second_start = W2_CHUNKS + 3
-        for r in range(second_start + HALVES * PASSES + 1):
+        rounds = 2 * W2_CHUNKS
+        groups = [(b, g) for b in range(len(BLOCKS)) for g in range(PASSES)]
+
+        def last_product(b, g):
+            return 2 * g + 1 if b == 0 else W2_CHUNKS + PASSES * (b - 1) + g
+
+        def tiles_of(r):
+            if r < W2_CHUNKS:
+                return 0, range(ROW_TILES * r, ROW_TILES * (r + 1))
+            b, g = divmod(r - W2_CHUNKS, PASSES)
+            return b + 1, range(PACK * g, PACK * (g + 1))
+
+        halves_at = {
+            4: [("h1", 2, 0)], 5: [("h1", 2, 1)], 7: [("h1", 3, 0)], 8: [("h1", 3, 1)],
+            9: [("w3", 0, 0), ("w3", 0, 1)], 10: [("w3", 1, 0), ("w3", 1, 1)],
+        }
+        parts = [(b, g, p) for b, g in groups for p in range(BLOCKS[b][1] // P)]
+        passes = [
+            (t, g) for b, g in groups for t in range(BLOCKS[b][0] // P, (BLOCKS[b][0] + BLOCKS[b][1]) // P)
+        ]
+        done = {"parts": 0, "groups": 0, "passes": 0, "tiles": 0}
+        pass_round = {}
+
+        def sines_round(b, g):
+            return last_product(b, g) + 1
+
+        def regroup_parts(r, engines):
+            for engine in engines:
+                if done["parts"] == len(parts):
+                    return
+                b, g, part = parts[done["parts"]]
+                if sines_round(b, g) + (1 if b == 0 else 0) > r:
+                    return
+                regroup(b, g, part, engine)
+                done["parts"] += 1
+
+        def quantise_groups(limit):
+            for n in range(limit):
+                if done["groups"] == len(groups):
+                    return
+                b, g = groups[done["groups"]]
+                if parts.index((b, g, BLOCKS[b][1] // P - 1)) >= done["parts"]:
+                    return
+                quantise_h2(b, g)
+                done["groups"] += 1
+
+        def run_passes(limit):
+            for n in range(limit):
+                if done["passes"] == len(passes):
+                    return
+                t, g = passes[done["passes"]]
+                b = 0 if t < TILES_PER_HALF else 1 + (t - TILES_PER_HALF) * P // QUARTER
+                if groups.index((b, g)) >= done["groups"]:
+                    return
+                second_product(t, g)
+                pass_round[t] = r
+                done["passes"] += 1
+
+        def finish_tiles():
+            while done["tiles"] < TOKEN_TILES and (
+                passes.index((done["tiles"], PASSES - 1)) < done["passes"] and pass_round[done["tiles"]] < r
+            ):
+                finish(done["tiles"])
+                done["tiles"] += 1
+
+        for r in range(rounds + 3):
             if r + 1 < W2_CHUNKS:
-                prepare_next()
-            elif r + 1 == W2_CHUNKS:
-                prepare_next()
-                prepare_next()
-            elif next_chunk[0] < len(chunks):
-                prepare_next()
-                if next_chunk[0] == len(chunks):
-                    load_residual()
-            if r - second_start in (PASSES, HALVES * PASSES):
-                finish((r - second_start) // PASSES - 1)
+                transpose_w2(r + 1)
+            for half in halves_at.get(r, []):
+                transpose_half(*half)
+            if 1 <= r <= W2_CHUNKS:
+                count_turns(0, 2 * r - 1)
+                take_off_turns(0, 2 * r - 2)
+                if r < W2_CHUNKS - 1:
+                    quantise_w2(2 * r + 2)
+                take_off_turns(0, 2 * r - 1)
+            elif r == 0:
+                quantise_w2(2)
+            if r + 1 < W2_CHUNKS:
+                quantise_w2(2 * r + 3)
+            for half in halves_at.get(r - 1, []):
+                quantise_half(*half)
+            if r == 7:
+                load_residual()
+            if 8 <= r < rounds:
+                add_b3(r - 8)
             if r < rounds:
-                first_product(r)
-                take_off_turns(r)
-            if 0 <= r - 1 < rounds:
-                sine(r - 1)
-            if 0 <= r - 2 < rounds and (r - 1) % rounds_per_group == 0:
-                scale_and_regroup(*divmod((r - 2) // rounds_per_group, PASSES))
-            if 0 <= r - 3 < rounds and r % rounds_per_group == 0:
-                quantise_h2(*divmod((r - 3) // rounds_per_group, PASSES))
-            if 0 <= r - second_start < HALVES * PASSES:
-                second_product(*divmod(r - second_start, PASSES))
+                b, tiles = tiles_of(r)
+                for m in tiles:
+                    first_product(b, m, second_quarter if r == 0 else None)
+            if 12 <= r < rounds:
+                run_passes(4 if r == 12 else 6)
+            if r < W2_CHUNKS:
+                count_turns(0, 2 * r)
+            elif r < rounds:
+                for m in tiles:
+                    count_turns(b, m)
+            if W2_CHUNKS <= r < rounds:
+                for bank in (2 * (r % PASSES), 2 * (r % PASSES) + 1):
+                    take_off_turns(b, bank)
+            quantise_groups(2 if r > 10 else 1)
+            finish_tiles()
+            if 1 <= r <= rounds:
+                sine_block, sine_tiles = tiles_of(r - 1)
+                for m in sine_tiles:
+                    sine(sine_block, m)
+            regroup_parts(r, "SVSV" if r >= rounds else "SSG" if r >= 10 else "SG" if r in (4, 7, 8, 9) else "G")
+            if r >= rounds:
+                run_passes(8)
+        assert done["tiles"] == TOKEN_TILES

@@ -342,9 +342,11 @@ def tile_transreachencoderlayer_pb_kernel(
             elif engine == "V":
                 nc.vector.tensor_scalar_mul(words[:, runs, :, :], sines[:, runs, :, :], gain[:, 0:1])
             else:
+                tokens = slice(part * P, (part + 1) * P)
                 nc.gpsimd.tensor_scalar(
-                    out=words[:, runs, :, :], in0=sines[:, runs, :, :], scalar1=gain[:, 0:1], scalar2=0.0,
-                    op0=ALU.mult, op1=ALU.add,
+                    out=h2_of[(block, group)][:, tokens, :],
+                    in0=angle_of[(block, group)][:, :, tokens].rearrange("p t n -> p n t"),
+                    scalar1=gain[:, 0:1], scalar2=0.0, op0=ALU.mult, op1=ALU.add,
                 )
 
         def quantise_h2(block, group):

@@ -19,6 +19,7 @@ K_PASS = P * PACK
 TOKENS = 1024
 D_FF = 2048
 D_MODEL = 512
+ROUNDS = 20
 PASSES = D_FF // K_PASS
 HALF = 512
 HALVES = TOKENS // HALF
@@ -31,7 +32,7 @@ TOKEN_TILES = TOKENS // P
 TILES_PER_HALF = HALF // P
 RAW_BUFS = 6
 SPLIT_LOADS = 4
-VECTOR_COPIES = 2
+VECTOR_COPIES = 3
 QUARTER = 256
 BLOCKS = ((0, HALF), (HALF, QUARTER), (HALF + QUARTER, QUARTER))
 BLOCK_BUFS = {HALF: (3, 2), QUARTER: (4, 3)}
@@ -125,11 +126,7 @@ def tile_transreachencoderlayer_pb_kernel(
 
         def add_b3(t):
             x1_raw = x1_raw_of[0]
-            for d in range(0, D_MODEL, P):
-                cols = slice(d, d + P)
-                nc.gpsimd.tensor_tensor(
-                    out=residual_of(t)[:, cols], in0=x1_raw[:, t, cols], in1=b3_rows[:, cols], op=ALU.add
-                )
+            nc.gpsimd.tensor_tensor(out=residual_of(t), in0=x1_raw[:, t, :], in1=b3_rows[:], op=ALU.add)
 
         grouped_of = {}
 
@@ -157,6 +154,13 @@ def tile_transreachencoderlayer_pb_kernel(
             copy(
                 out=target[:, 2 * j : 2 * j + 2, r, :, :], in_=bank[:].rearrange("q k u i -> q k i u")
             )
+
+        waits = keep.tile([P, ROUNDS], U32)
+        last_codes = {}
+
+        def wait_for_quantises(r):
+            if r in last_codes:
+                nc.gpsimd.tensor_copy(out=waits[:, r : r + 1], in_=last_codes[r])
 
         def quantise_w2(m):
             c, r = divmod(m, ROW_TILES)
@@ -198,11 +202,6 @@ def tile_transreachencoderlayer_pb_kernel(
                 transpose_bank(i, r, j)
             if j == 1:
                 load(i + RAW_BUFS)
-
-        def prepare_h1(c):
-            for j in range(2):
-                transpose_half("h1", c, j)
-                quantise_half("h1", c, j)
 
         a_bf = keep.tile([P, 1], BF16)
         b_bf = keep.tile([P, 1], BF16)
@@ -386,24 +385,24 @@ def tile_transreachencoderlayer_pb_kernel(
                     in_=ffn_b2.rearrange("(c p e) -> p c e", p=P, e=2),
                 )
         wave_constants()
-        first_quarter, second_quarter = (0, QUARTER), (QUARTER, HALF)
-        prepare_h1(0)
+        transpose_half("h1", 0, 0)
+        quantise_half("h1", 0, 0)
+        transpose_half("h1", 0, 1)
+        quantise_half("h1", 0, 1)
         newton_step()
         transpose_w2(0)
         quantise_w2(0)
+        newton_step()
+        transpose_half("h1", 1, 0)
         quantise_w2(1)
+        quantise_half("h1", 1, 0)
         newton_step()
-        for m in range(ROW_TILES):
-            first_product(0, m, first_quarter)
-        prepare_h1(1)
-        newton_step()
+        transpose_half("h1", 1, 1)
+        quantise_half("h1", 1, 1)
         biases()
 
-        rounds = 2 * W2_CHUNKS
+        products = 2 * W2_CHUNKS
         groups = [(b, g) for b in range(len(BLOCKS)) for g in range(PASSES)]
-
-        def last_product(b, g):
-            return 2 * g + 1 if b == 0 else W2_CHUNKS + PASSES * (b - 1) + g
 
         def tiles_of(r):
             if r < W2_CHUNKS:
@@ -411,31 +410,29 @@ def tile_transreachencoderlayer_pb_kernel(
             b, g = divmod(r - W2_CHUNKS, PASSES)
             return b + 1, range(PACK * g, PACK * (g + 1))
 
-        halves_at = {
-            4: [("h1", 2, 0)], 5: [("h1", 2, 1)], 7: [("h1", 3, 0)], 8: [("h1", 3, 1)],
-            9: [("w3", 0, 0), ("w3", 0, 1)], 10: [("w3", 1, 0), ("w3", 1, 1)],
-        }
-        parts = [(b, g, p) for b, g in groups for p in range(BLOCKS[b][1] // P)]
+        def last_product(b, g):
+            return 2 * g + 1 if b == 0 else W2_CHUNKS + PASSES * (b - 1) + g
+
+        halves_at = {5: [("h1", 2, 0)], 6: [("h1", 2, 1)]}
+        for r, (kind, c) in ((8, ("h1", 3)), (9, ("w3", 0)), (10, ("w3", 1))):
+            halves_at[r] = [(kind, c, 0), (kind, c, 1)]
+        parts = [(b, g, part) for b, g in groups for part in range(BLOCKS[b][1] // P)]
         passes = [
             (t, g) for b, g in groups for t in range(BLOCKS[b][0] // P, (BLOCKS[b][0] + BLOCKS[b][1]) // P)
         ]
         done = {"parts": 0, "groups": 0, "passes": 0, "tiles": 0}
-        pass_round = {}
-
-        def sines_round(b, g):
-            return last_product(b, g) + 1
 
         def regroup_parts(r, engines):
             for engine in engines:
                 if done["parts"] == len(parts):
                     return
                 b, g, part = parts[done["parts"]]
-                if sines_round(b, g) + (1 if b == 0 else 0) > r:
+                if last_product(b, g) + (2 if b == 0 else 1) > r:
                     return
                 regroup(b, g, part, engine)
                 done["parts"] += 1
 
-        def quantise_groups(limit):
+        def quantise_groups(r, limit):
             for n in range(limit):
                 if done["groups"] == len(groups):
                     return
@@ -443,6 +440,7 @@ def tile_transreachencoderlayer_pb_kernel(
                 if parts.index((b, g, BLOCKS[b][1] // P - 1)) >= done["parts"]:
                     return
                 quantise_h2(b, g)
+                last_codes[r] = h2_codes[:, g, BLOCKS[b][0] : BLOCKS[b][0] + 1]
                 done["groups"] += 1
 
         def run_passes(limit):
@@ -454,58 +452,50 @@ def tile_transreachencoderlayer_pb_kernel(
                 if groups.index((b, g)) >= done["groups"]:
                     return
                 second_product(t, g)
-                pass_round[t] = r
                 done["passes"] += 1
 
         def finish_tiles():
             while done["tiles"] < TOKEN_TILES and (
-                passes.index((done["tiles"], PASSES - 1)) < done["passes"] and pass_round[done["tiles"]] < r
+                passes.index((done["tiles"], PASSES - 1)) < done["passes"]
             ):
                 finish(done["tiles"])
                 done["tiles"] += 1
 
-        for r in range(rounds + 3):
+        for r in range(ROUNDS):
             if r + 1 < W2_CHUNKS:
                 transpose_w2(r + 1)
             for half in halves_at.get(r, []):
                 transpose_half(*half)
-            if 1 <= r <= W2_CHUNKS:
-                count_turns(0, 2 * r - 1)
-                take_off_turns(0, 2 * r - 2)
-                if r < W2_CHUNKS - 1:
-                    quantise_w2(2 * r + 2)
-                take_off_turns(0, 2 * r - 1)
-            elif r == 0:
-                quantise_w2(2)
+            quantise_groups(r, 2)
             if r + 1 < W2_CHUNKS:
-                quantise_w2(2 * r + 3)
-            for half in halves_at.get(r - 1, []):
-                quantise_half(*half)
-            if r == 7:
+                for m in range(ROW_TILES * (r + 1), ROW_TILES * (r + 2)):
+                    quantise_w2(m)
+                last_codes[r] = w2_codes[:, m, PASSES - 1, P - 1 : P]
+            for kind, c, j in halves_at.get(r - 1, []):
+                quantise_half(kind, c, j)
+                last_codes[r] = (h1_codes[:, 1, 2 * j + 1, 256 * (c - 2) : 256 * (c - 2) + 1] if kind == "h1" else w3_codes[:, 2 * j + 1, 256 * c : 256 * c + 1])
+            wait_for_quantises(r)
+            if r == 5:
                 load_residual()
-            if 8 <= r < rounds:
+            if 8 <= r < 8 + TOKEN_TILES:
                 add_b3(r - 8)
-            if r < rounds:
+            if r < products:
                 b, tiles = tiles_of(r)
+                run_passes({14: 4, 15: 2}.get(r, 0))
                 for m in tiles:
-                    first_product(b, m, second_quarter if r == 0 else None)
-            if 12 <= r < rounds:
-                run_passes(4 if r == 12 else 6)
-            if r < W2_CHUNKS:
-                count_turns(0, 2 * r)
-            elif r < rounds:
+                    first_product(b, m)
+                run_passes({12: 4, 13: 6}.get(r, 0))
                 for m in tiles:
                     count_turns(b, m)
-            if W2_CHUNKS <= r < rounds:
-                for bank in (2 * (r % PASSES), 2 * (r % PASSES) + 1):
-                    take_off_turns(b, bank)
-            quantise_groups(2 if r > 10 else 1)
+                bank = tiles[0] * BLOCKS[b][1] // HALF
+                take_off_turns(b, bank)
+                take_off_turns(b, bank + 1)
             finish_tiles()
-            if 1 <= r <= rounds:
-                sine_block, sine_tiles = tiles_of(r - 1)
-                for m in sine_tiles:
-                    sine(sine_block, m)
-            regroup_parts(r, "SVSV" if r >= rounds else "SSG" if r >= 10 else "SG" if r in (4, 7, 8, 9) else "G")
-            if r >= rounds:
-                run_passes(8)
+            if 1 <= r <= products:
+                b, tiles = tiles_of(r - 1)
+                for m in tiles:
+                    sine(b, m)
+            regroup_parts(r, "GG" if r < W2_CHUNKS else "GSS" if r < products else "SV")
+            if r >= products:
+                run_passes(len(passes))
         assert done["tiles"] == TOKEN_TILES

@@ -185,6 +185,14 @@ def tile_transreachencoderlayer_pb_kernel(
                 in_=grouped[:, k * CHUNK_ROWS * PACK : (k + 1) * CHUNK_ROWS * PACK],
             )
 
+        idle_words = keep.tile([P, HALF], BF16)
+        nc.vector.memset(idle_words[:], 0.0)
+
+        def warm_up(n):
+            for k in range(n):
+                bank = sums_pool.tile([P, HALF], F32, tag="sums")
+                nc.tensor.matmul(bank[:], lhsT=idle_words[:, 0:P], rhs=idle_words[:], start=True, stop=True)
+
         def quantise_half(kind, c, j):
             quantise_moving(kind, c, 2 * j)
             quantise_moving(kind, c, 2 * j + 1)
@@ -385,19 +393,25 @@ def tile_transreachencoderlayer_pb_kernel(
                     in_=ffn_b2.rearrange("(c p e) -> p c e", p=P, e=2),
                 )
         wave_constants()
+        warm_up(12)
         transpose_half("h1", 0, 0)
+        warm_up(3)
         quantise_half("h1", 0, 0)
         transpose_half("h1", 0, 1)
+        warm_up(3)
         quantise_half("h1", 0, 1)
         newton_step()
         transpose_w2(0)
+        warm_up(3)
         quantise_w2(0)
         newton_step()
         transpose_half("h1", 1, 0)
+        warm_up(3)
         quantise_w2(1)
         quantise_half("h1", 1, 0)
         newton_step()
         transpose_half("h1", 1, 1)
+        warm_up(3)
         quantise_half("h1", 1, 1)
         biases()
 

@@ -509,7 +509,7 @@ def tile_transreachencoderlayer_pb_kernel(
                 b, tiles = tiles_of(r - 1)
                 for m in tiles:
                     sine(b, m)
-            regroup_parts(r, "GG" if r < W2_CHUNKS else "GSS" if r < products else "SV")
+            regroup_parts(r, "SV" if r < W2_CHUNKS else "SSV" if r < products else "SV")
             if r >= products:
                 run_passes(len(passes))
         assert done["tiles"] == TOKEN_TILES

@@ -19,7 +19,7 @@ K_PASS = P * PACK
 TOKENS = 1024
 D_FF = 2048
 D_MODEL = 512
-ROUNDS = 20
+ROUNDS = 26
 PASSES = D_FF // K_PASS
 HALF = 512
 HALVES = TOKENS // HALF
@@ -34,8 +34,11 @@ RAW_BUFS = 6
 SPLIT_LOADS = 4
 VECTOR_COPIES = 3
 QUARTER = 256
-BLOCKS = ((0, HALF), (HALF, QUARTER), (HALF + QUARTER, QUARTER))
-BLOCK_BUFS = {HALF: (3, 2), QUARTER: (4, 3)}
+UNITS = (
+    [(0, HALF, g) for g in range(PASSES)]
+    + [(HALF + QUARTER * q, QUARTER, g) for q in range(2) for g in range(PASSES)]
+)
+UNIT_BUFS = {HALF: (3, 2), QUARTER: (4, 2)}
 NEWTON_STEPS = 3
 RUN = 4
 TWO_PI = 2.0 * math.pi
@@ -155,13 +158,6 @@ def tile_transreachencoderlayer_pb_kernel(
                 out=target[:, 2 * j : 2 * j + 2, r, :, :], in_=bank[:].rearrange("q k u i -> q k i u")
             )
 
-        waits = keep.tile([P, ROUNDS], U32)
-        last_codes = {}
-
-        def wait_for_quantises(r):
-            if r in last_codes:
-                nc.gpsimd.tensor_copy(out=waits[:, r : r + 1], in_=last_codes[r])
-
         def quantise_w2(m):
             c, r = divmod(m, ROW_TILES)
             nc.vector.quantize_mx(
@@ -280,67 +276,65 @@ def tile_transreachencoderlayer_pb_kernel(
         h2_of = {}
         acc_of = {}
 
-        def first_product(block, m, cols=None):
-            first, width = BLOCKS[block]
-            per_bank = HALF // width
-            key = (block, m // per_bank)
+        def bank_of(u, m):
+            first, width, group = UNITS[u]
+            bank, place = divmod(m % PACK, HALF // width)
+            return (u, bank), slice(place * width, (place + 1) * width)
+
+        def first_product(u, m):
+            first, width, group = UNITS[u]
+            key, cols = bank_of(u, m)
             if key not in sums_of:
                 sums_tile = sums_pool.tile([P, HALF], F32, tag="sums")
                 sums_of[key] = sums_tile
-            base = (m % per_bank) * width
-            lo, hi = cols or (0, width)
             half, start_col = divmod(first, HALF)
+            tokens = slice(start_col, start_col + width)
             for k in range(PASSES):
                 nc.tensor.matmul_mx(
-                    out=sums_of[key][:, base + lo : base + hi],
+                    out=sums_of[key][:, cols],
                     lhsT=w2_codes[:, m, k, :].bitcast(FP8X4),
                     lhsT_scale=w2_scales[:, m, k, :],
-                    rhs=h1_codes[:, half, k, start_col + lo : start_col + hi].bitcast(FP8X4),
-                    rhs_scale=h1_scales[:, half, k, start_col + lo : start_col + hi],
+                    rhs=h1_codes[:, half, k, tokens].bitcast(FP8X4),
+                    rhs_scale=h1_scales[:, half, k, tokens],
                     start=(k == 0),
                     stop=(k == PASSES - 1),
                 )
 
-        def count_turns(block, m):
-            first, width = BLOCKS[block]
-            per_bank = HALF // width
-            key = (block, m // per_bank)
+        def count_turns(u, m):
+            key, cols = bank_of(u, m)
             if key not in turns_of:
                 turns_tile = turns_pool.tile([P, HALF], I32, tag="turns")
                 turns_of[key] = turns_tile
-            cols = slice((m % per_bank) * width, (m % per_bank + 1) * width)
             nc.vector.tensor_scalar(
                 out=turns_of[key][:, cols], in0=sums_of[key][:, cols], scalar1=1.0 / TWO_PI,
                 scalar2=bias_turns[:, m : m + 1], op0=ALU.mult, op1=ALU.add,
             )
 
-        def take_off_turns(block, b):
-            first, width = BLOCKS[block]
-            per_bank = HALF // width
-            group, place = divmod(b * per_bank, PACK)
-            if (block, group) not in angle_of:
-                angle_tile = angle_pool.tile([P, PACK, width], F32, tag="angle%d" % width, bufs=BLOCK_BUFS[width][0])
-                angle_of[(block, group)] = angle_tile
+        def take_off_turns(u, bank):
+            first, width, group = UNITS[u]
+            places = slice(bank * (HALF // width), (bank + 1) * (HALF // width))
+            if u not in angle_of:
+                angle_tile = angle_pool.tile([P, PACK, width], F32, tag="angle%d" % width, bufs=UNIT_BUFS[width][0])
+                angle_of[u] = angle_tile
             nc.vector.scalar_tensor_tensor(
-                out=angle_of[(block, group)][:, place : place + per_bank, :].rearrange("p t n -> p (t n)"),
-                in0=turns_of[(block, b)][:], scalar=-TWO_PI,
-                in1=sums_of[(block, b)][:], op0=ALU.mult, op1=ALU.add,
+                out=angle_of[u][:, places, :].rearrange("p t n -> p (t n)"),
+                in0=turns_of[(u, bank)][:], scalar=-TWO_PI,
+                in1=sums_of[(u, bank)][:], op0=ALU.mult, op1=ALU.add,
             )
 
-        def sine(block, m):
-            group, place = divmod(m, PACK)
-            angle = angle_of[(block, group)]
+        def sine(u, m):
+            angle = angle_of[u]
             nc.scalar.activation(
-                out=angle[:, place, :], in_=angle[:, place, :], func=ACT.Sin, bias=bias[:, m : m + 1]
+                out=angle[:, m % PACK, :], in_=angle[:, m % PACK, :], func=ACT.Sin, bias=bias[:, m : m + 1]
             )
 
-        def regroup(block, group, part, engine):
-            first, width = BLOCKS[block]
-            if (block, group) not in h2_of:
-                h2_tile = h2_pool.tile([P, width, PACK], BF16, tag="h2%d" % width, bufs=BLOCK_BUFS[width][1], align_bytes=64)
-                h2_of[(block, group)] = h2_tile
-            sines = angle_of[(block, group)][:].rearrange("p t (c i) -> p c t i", i=RUN)
-            words = h2_of[(block, group)][:].rearrange("p (c i) t -> p c t i", i=RUN)
+        def regroup(u, part, engine):
+            first, width, group = UNITS[u]
+            if u not in h2_of:
+                h2_tile = h2_pool.tile([P, width, PACK], BF16, tag="h2%d" % width, bufs=UNIT_BUFS[width][1], align_bytes=64)
+                h2_of[u] = h2_tile
+            sines = angle_of[u][:].rearrange("p t (c i) -> p c t i", i=RUN)
+            words = h2_of[u][:].rearrange("p (c i) t -> p c t i", i=RUN)
             runs = slice(part * P // RUN, (part + 1) * P // RUN)
             if engine == "S":
                 nc.scalar.activation(
@@ -351,17 +345,17 @@ def tile_transreachencoderlayer_pb_kernel(
             else:
                 tokens = slice(part * P, (part + 1) * P)
                 nc.gpsimd.tensor_scalar(
-                    out=h2_of[(block, group)][:, tokens, :],
-                    in0=angle_of[(block, group)][:, :, tokens].rearrange("p t n -> p n t"),
+                    out=h2_of[u][:, tokens, :],
+                    in0=angle_of[u][:, :, tokens].rearrange("p t n -> p n t"),
                     scalar1=gain[:, 0:1], scalar2=0.0, op0=ALU.mult, op1=ALU.add,
                 )
 
-        def quantise_h2(block, group):
-            first, width = BLOCKS[block]
+        def quantise_h2(u):
+            first, width, group = UNITS[u]
             nc.vector.quantize_mx(
                 out=h2_codes[:, group, first : first + width].bitcast(FP8X4),
                 scales=h2_scales[:, group, first : first + width],
-                in_=h2_of[(block, group)][:].rearrange("p n t -> p (n t)"),
+                in_=h2_of[u][:].rearrange("p n t -> p (n t)"),
             )
 
         def second_product(t, group):
@@ -415,64 +409,55 @@ def tile_transreachencoderlayer_pb_kernel(
         quantise_half("h1", 1, 1)
         biases()
 
-        products = 2 * W2_CHUNKS
-        groups = [(b, g) for b in range(len(BLOCKS)) for g in range(PASSES)]
-
-        def tiles_of(r):
-            if r < W2_CHUNKS:
-                return 0, range(ROW_TILES * r, ROW_TILES * (r + 1))
-            b, g = divmod(r - W2_CHUNKS, PASSES)
-            return b + 1, range(PACK * g, PACK * (g + 1))
-
-        def last_product(b, g):
-            return 2 * g + 1 if b == 0 else W2_CHUNKS + PASSES * (b - 1) + g
-
-        halves_at = {5: [("h1", 2, 0)], 6: [("h1", 2, 1)]}
-        for r, (kind, c) in ((8, ("h1", 3)), (9, ("w3", 0)), (10, ("w3", 1))):
-            halves_at[r] = [(kind, c, 0), (kind, c, 1)]
-        parts = [(b, g, part) for b, g in groups for part in range(BLOCKS[b][1] // P)]
-        passes = [
-            (t, g) for b, g in groups for t in range(BLOCKS[b][0] // P, (BLOCKS[b][0] + BLOCKS[b][1]) // P)
+        rounds = [
+            (u, range(PACK * g + first, PACK * g + first + n))
+            for u, (token, width, g) in enumerate(UNITS)
+            for n in (PACK * QUARTER // width,)
+            for first in range(0, PACK, n)
         ]
-        done = {"parts": 0, "groups": 0, "passes": 0, "tiles": 0}
+        products = len(rounds)
+        last_product = {u: r for r, (u, tiles) in enumerate(rounds)}
+
+        halves_at = {5: [("h1", 2, 0)], 6: [("h1", 2, 1)], 7: [("h1", 3, 0)], 8: [("h1", 3, 1)], 9: [("w3", 0, 0)], 10: [("w3", 0, 1), ("w3", 1, 0)], 11: [("w3", 1, 1)]}
+        parts = [(u, part) for u, (token, width, g) in enumerate(UNITS) for part in range(width // P)]
+        passes = [(t, u) for u, (token, width, g) in enumerate(UNITS) for t in range(token // P, (token + width) // P)]
+        done = {"parts": 0, "units": 0, "passes": 0, "tiles": 0}
 
         def regroup_parts(r, engines):
             for engine in engines:
                 if done["parts"] == len(parts):
                     return
-                b, g, part = parts[done["parts"]]
-                if last_product(b, g) + (2 if b == 0 else 1) > r:
+                u, part = parts[done["parts"]]
+                if last_product[u] + (2 if UNITS[u][1] == HALF else 1) > r:
                     return
-                regroup(b, g, part, engine)
+                regroup(u, part, engine)
                 done["parts"] += 1
 
-        def quantise_groups(r, limit):
+        def quantise_units(r, limit):
             for n in range(limit):
-                if done["groups"] == len(groups):
+                u = done["units"]
+                if u == len(UNITS) or parts.index((u, UNITS[u][1] // P - 1)) >= done["parts"]:
                     return
-                b, g = groups[done["groups"]]
-                if parts.index((b, g, BLOCKS[b][1] // P - 1)) >= done["parts"]:
-                    return
-                quantise_h2(b, g)
-                last_codes[r] = h2_codes[:, g, BLOCKS[b][0] : BLOCKS[b][0] + 1]
-                done["groups"] += 1
+                quantise_h2(u)
+                done["units"] += 1
 
         def run_passes(limit):
             for n in range(limit):
                 if done["passes"] == len(passes):
                     return
-                t, g = passes[done["passes"]]
-                b = 0 if t < TILES_PER_HALF else 1 + (t - TILES_PER_HALF) * P // QUARTER
-                if groups.index((b, g)) >= done["groups"]:
+                t, u = passes[done["passes"]]
+                if u >= done["units"]:
                     return
-                second_product(t, g)
+                second_product(t, UNITS[u][2])
+                if UNITS[u][2] == PASSES - 1:
+                    complete.append(t)
                 done["passes"] += 1
 
+        complete = []
+
         def finish_tiles():
-            while done["tiles"] < TOKEN_TILES and (
-                passes.index((done["tiles"], PASSES - 1)) < done["passes"]
-            ):
-                finish(done["tiles"])
+            for t in complete[done["tiles"] :]:
+                finish(t)
                 done["tiles"] += 1
 
         for r in range(ROUNDS):
@@ -480,36 +465,32 @@ def tile_transreachencoderlayer_pb_kernel(
                 transpose_w2(r + 1)
             for half in halves_at.get(r, []):
                 transpose_half(*half)
-            quantise_groups(r, 2)
+            quantise_units(r, 3)
             if r + 1 < W2_CHUNKS:
                 for m in range(ROW_TILES * (r + 1), ROW_TILES * (r + 2)):
                     quantise_w2(m)
-                last_codes[r] = w2_codes[:, m, PASSES - 1, P - 1 : P]
             for kind, c, j in halves_at.get(r - 1, []):
                 quantise_half(kind, c, j)
-                last_codes[r] = (h1_codes[:, 1, 2 * j + 1, 256 * (c - 2) : 256 * (c - 2) + 1] if kind == "h1" else w3_codes[:, 2 * j + 1, 256 * c : 256 * c + 1])
-            wait_for_quantises(r)
-            if r == 5:
+            if r == 7:
                 load_residual()
-            if 8 <= r < 8 + TOKEN_TILES:
-                add_b3(r - 8)
+            for t in range(2 * (r - 10), 2 * (r - 9)) if 10 <= r < 14 else ():
+                add_b3(t)
             if r < products:
-                b, tiles = tiles_of(r)
-                run_passes({14: 4, 15: 2}.get(r, 0))
+                u, tiles = rounds[r]
+                run_passes({14: 4}.get(r, 0))
                 for m in tiles:
-                    first_product(b, m)
-                run_passes({12: 4, 13: 6}.get(r, 0))
+                    first_product(u, m)
+                run_passes({12: 6, 13: 4, 15: 4}.get(r, 0))
                 for m in tiles:
-                    count_turns(b, m)
-                bank = tiles[0] * BLOCKS[b][1] // HALF
-                take_off_turns(b, bank)
-                take_off_turns(b, bank + 1)
+                    count_turns(u, m)
+                for bank in (0, 1) if len(tiles) == PACK else (tiles[0] % PACK, tiles[1] % PACK):
+                    take_off_turns(u, bank)
             finish_tiles()
             if 1 <= r <= products:
-                b, tiles = tiles_of(r - 1)
+                u, tiles = rounds[r - 1]
                 for m in tiles:
-                    sine(b, m)
-            regroup_parts(r, "SV" if r < W2_CHUNKS else "SSV" if r < products else "SV")
+                    sine(u, m)
+            regroup_parts(r, "GV" if r < 6 else "SV" if r < W2_CHUNKS else "SSG" if r < 11 else "SS" if r < products else "SVSV")
             if r >= products:
                 run_passes(len(passes))
         assert done["tiles"] == TOKEN_TILES

@@ -387,7 +387,7 @@ def tile_transreachencoderlayer_pb_kernel(
                     in_=ffn_b2.rearrange("(c p e) -> p c e", p=P, e=2),
                 )
         wave_constants()
-        warm_up(12)
+        warm_up(7)
         transpose_half("h1", 0, 0)
         warm_up(3)
         quantise_half("h1", 0, 0)
@@ -418,7 +418,7 @@ def tile_transreachencoderlayer_pb_kernel(
         products = len(rounds)
         last_product = {u: r for r, (u, tiles) in enumerate(rounds)}
 
-        halves_at = {5: [("h1", 2, 0)], 6: [("h1", 2, 1)], 7: [("h1", 3, 0)], 8: [("h1", 3, 1)], 9: [("w3", 0, 0)], 10: [("w3", 0, 1), ("w3", 1, 0)], 11: [("w3", 1, 1)]}
+        halves_at = {5: [("h1", 2, 0)], 6: [("h1", 2, 1)], 8: [("h1", 3, 0), ("h1", 3, 1)], 9: [("w3", 0, 0), ("w3", 0, 1)], 10: [("w3", 1, 0)], 11: [("w3", 1, 1)]}
         parts = [(u, part) for u, (token, width, g) in enumerate(UNITS) for part in range(width // P)]
         passes = [(t, u) for u, (token, width, g) in enumerate(UNITS) for t in range(token // P, (token + width) // P)]
         done = {"parts": 0, "units": 0, "passes": 0, "tiles": 0}
@@ -471,10 +471,10 @@ def tile_transreachencoderlayer_pb_kernel(
                     quantise_w2(m)
             for kind, c, j in halves_at.get(r - 1, []):
                 quantise_half(kind, c, j)
-            if r == 7:
+            if r == 6:
                 load_residual()
-            for t in range(2 * (r - 10), 2 * (r - 9)) if 10 <= r < 14 else ():
-                add_b3(t)
+            if 8 <= r < 8 + TOKEN_TILES:
+                add_b3(r - 8)
             if r < products:
                 u, tiles = rounds[r]
                 run_passes({14: 4}.get(r, 0))
@@ -490,7 +490,7 @@ def tile_transreachencoderlayer_pb_kernel(
                 u, tiles = rounds[r - 1]
                 for m in tiles:
                     sine(u, m)
-            regroup_parts(r, "GV" if r < 6 else "SV" if r < W2_CHUNKS else "SSG" if r < 11 else "SS" if r < products else "SVSV")
+            regroup_parts(r, "GV" if r < 6 else "GG" if r < W2_CHUNKS else "GSS" if r < products else "SVSV")
             if r >= products:
                 run_passes(len(passes))
         assert done["tiles"] == TOKEN_TILES

@@ -67,8 +67,8 @@ def tile_transreachencoderlayer_pb_kernel(
         sums_pool = ctx.enter_context(tc.psum_pool(name="sums", bufs=4))
         ctx.enter_context(tc.manual_schedule())
 
-        h1_codes = keep.tile([P, HALVES, PASSES, HALF], U32, align_bytes=64)
-        h1_scales = keep.tile([P, HALVES, PASSES, HALF], U8, align_bytes=64)
+        h1_codes = keep.tile([P, TOKENS // QUARTER, PASSES, QUARTER], U32, align_bytes=64)
+        h1_scales = keep.tile([P, TOKENS // QUARTER, PASSES, QUARTER], U8, align_bytes=64)
         w2_codes = keep.tile([P, FEATURE_TILES, PASSES, P], U32, align_bytes=64)
         w2_scales = keep.tile([P, FEATURE_TILES, PASSES, P], U8, align_bytes=64)
         w3_codes = keep.tile([P, PASSES, D_MODEL], U32, align_bytes=64)
@@ -168,13 +168,8 @@ def tile_transreachencoderlayer_pb_kernel(
 
         def quantise_moving(kind, c, k):
             grouped = grouped_of[position[(kind, c)]]
-            if kind == "h1":
-                half, part = divmod(c, HALF // CHUNK_ROWS)
-                cols = slice(part * CHUNK_ROWS, (part + 1) * CHUNK_ROWS)
-                codes, scales = h1_codes[:, half, k, cols], h1_scales[:, half, k, cols]
-            else:
-                cols = slice(c * CHUNK_ROWS, (c + 1) * CHUNK_ROWS)
-                codes, scales = w3_codes[:, k, cols], w3_scales[:, k, cols]
+            cols = slice(c * CHUNK_ROWS, (c + 1) * CHUNK_ROWS)
+            codes, scales = w3_codes[:, k, cols], w3_scales[:, k, cols]
             nc.vector.quantize_mx(
                 out=codes.bitcast(FP8X4),
                 scales=scales,
@@ -190,6 +185,13 @@ def tile_transreachencoderlayer_pb_kernel(
                 nc.tensor.matmul(bank[:], lhsT=idle_words[:, 0:P], rhs=idle_words[:], start=True, stop=True)
 
         def quantise_half(kind, c, j):
+            if kind == "h1":
+                nc.vector.quantize_mx(
+                    out=h1_codes[:, c, 2 * j : 2 * j + 2, :].rearrange("p k n -> p (k n)").bitcast(FP8X4),
+                    scales=h1_scales[:, c, 2 * j : 2 * j + 2, :].rearrange("p k n -> p (k n)"),
+                    in_=grouped_of[position[(kind, c)]][:, j * D_FF : (j + 1) * D_FF],
+                )
+                return
             quantise_moving(kind, c, 2 * j)
             quantise_moving(kind, c, 2 * j + 1)
 
@@ -287,18 +289,18 @@ def tile_transreachencoderlayer_pb_kernel(
             if key not in sums_of:
                 sums_tile = sums_pool.tile([P, HALF], F32, tag="sums")
                 sums_of[key] = sums_tile
-            half, start_col = divmod(first, HALF)
-            tokens = slice(start_col, start_col + width)
-            for k in range(PASSES):
-                nc.tensor.matmul_mx(
-                    out=sums_of[key][:, cols],
-                    lhsT=w2_codes[:, m, k, :].bitcast(FP8X4),
-                    lhsT_scale=w2_scales[:, m, k, :],
-                    rhs=h1_codes[:, half, k, tokens].bitcast(FP8X4),
-                    rhs_scale=h1_scales[:, half, k, tokens],
-                    start=(k == 0),
-                    stop=(k == PASSES - 1),
-                )
+            for n in range(width // QUARTER):
+                q = first // QUARTER + n
+                for k in range(PASSES):
+                    nc.tensor.matmul_mx(
+                        out=sums_of[key][:, cols.start + n * QUARTER : cols.start + (n + 1) * QUARTER],
+                        lhsT=w2_codes[:, m, k, :].bitcast(FP8X4),
+                        lhsT_scale=w2_scales[:, m, k, :],
+                        rhs=h1_codes[:, q, k, :].bitcast(FP8X4),
+                        rhs_scale=h1_scales[:, q, k, :],
+                        start=(k == 0),
+                        stop=(k == PASSES - 1),
+                    )
 
         def count_turns(u, m):
             key, cols = bank_of(u, m)
@@ -352,11 +354,13 @@ def tile_transreachencoderlayer_pb_kernel(
 
         def quantise_h2(u):
             first, width, group = UNITS[u]
-            nc.vector.quantize_mx(
-                out=h2_codes[:, group, first : first + width].bitcast(FP8X4),
-                scales=h2_scales[:, group, first : first + width],
-                in_=h2_of[u][:].rearrange("p n t -> p (n t)"),
-            )
+            step = P if u == len(UNITS) - 1 else width
+            for n in range(0, width, step):
+                nc.vector.quantize_mx(
+                    out=h2_codes[:, group, first + n : first + n + step].bitcast(FP8X4),
+                    scales=h2_scales[:, group, first + n : first + n + step],
+                    in_=h2_of[u][:, n : n + step, :].rearrange("p n t -> p (n t)"),
+                )
 
         def second_product(t, group):
             cols = slice(t * P, (t + 1) * P)
@@ -463,8 +467,9 @@ def tile_transreachencoderlayer_pb_kernel(
         for r in range(ROUNDS):
             if r + 1 < W2_CHUNKS:
                 transpose_w2(r + 1)
-            for half in halves_at.get(r, []):
-                transpose_half(*half)
+            if r >= W2_CHUNKS:
+                for half in halves_at.get(r, []):
+                    transpose_half(*half)
             quantise_units(r, 3)
             if r + 1 < W2_CHUNKS:
                 for m in range(ROW_TILES * (r + 1), ROW_TILES * (r + 2)):
@@ -480,6 +485,9 @@ def tile_transreachencoderlayer_pb_kernel(
                 run_passes({14: 4}.get(r, 0))
                 for m in tiles:
                     first_product(u, m)
+                    if r < W2_CHUNKS and m == tiles[0]:
+                        for half in halves_at.get(r, []):
+                            transpose_half(*half)
                 run_passes({12: 6, 13: 4, 15: 4}.get(r, 0))
                 for m in tiles:
                     count_turns(u, m)

import math
from contextlib import ExitStack

import concourse.mybir as mybir
from concourse.masks import make_identity

F32 = mybir.dt.float32
BF16 = mybir.dt.bfloat16
I32 = mybir.dt.int32
U32 = mybir.dt.uint32
U8 = mybir.dt.uint8
FP8X4 = mybir.dt.float8_e4m3fn_x4
ALU = mybir.AluOpType
ACT = mybir.ActivationFunctionType

P = 128
PACK = 4
K_PASS = P * PACK
TOKENS = 1024
D_FF = 2048
D_MODEL = 512
ROUNDS = 26
PASSES = D_FF // K_PASS
HALF = 512
HALVES = TOKENS // HALF
ROW_TILES = 2
CHUNK_ROWS = ROW_TILES * P
WORDS = D_FF // 2
FEATURE_TILES = D_FF // P
W2_CHUNKS = D_FF // CHUNK_ROWS
TOKEN_TILES = TOKENS // P
TILES_PER_HALF = HALF // P
RAW_BUFS = 6
SPLIT_LOADS = 4
VECTOR_COPIES = 3
QUARTER = 256
UNITS = (
    [(0, HALF, g) for g in range(PASSES)]
    + [(HALF + QUARTER * q, QUARTER, g) for q in range(2) for g in range(PASSES)]
)
UNIT_BUFS = {HALF: (3, 2), QUARTER: (4, 2)}
NEWTON_STEPS = 3
RUN = 4
TWO_PI = 2.0 * math.pi
HALF_PI = 0.5 * math.pi
TINY = 1e-36

FLOPS = 2 * TOKENS * D_FF * D_FF + 2 * TOKENS * D_FF * D_MODEL


def tile_transreachencoderlayer_pb_kernel(
    tc, h1, x1, ffn_w2, ffn_b2, ffn_a2w1, ffn_a2w2, ffn_w3, ffn_b3, out
):
    nc = tc.nc
    h1_rows = h1.rearrange("b s k -> (b s) k")
    x1_rows = x1.rearrange("b s d -> (b s) d")
    out_rows = out.rearrange("b s d -> (b s) d")

    with ExitStack() as ctx:
        keep = ctx.enter_context(tc.tile_pool(name="keep", bufs=1))
        raw_pool = ctx.enter_context(tc.tile_pool(name="raw", bufs=RAW_BUFS))
        grouped_pool = ctx.enter_context(tc.tile_pool(name="grouped", bufs=3))
        turns_pool = ctx.enter_context(tc.tile_pool(name="turns", bufs=4))
        angle_pool = ctx.enter_context(tc.tile_pool(name="angle", bufs=3))
        h2_pool = ctx.enter_context(tc.tile_pool(name="h2", bufs=2))
        bank_pool = ctx.enter_context(tc.psum_pool(name="bank", bufs=4))
        sums_pool = ctx.enter_context(tc.psum_pool(name="sums", bufs=4))
        ctx.enter_context(tc.manual_schedule())

        h1_codes = keep.tile([P, TOKENS // QUARTER, PASSES, QUARTER], U32, align_bytes=64)
        h1_scales = keep.tile([P, TOKENS // QUARTER, PASSES, QUARTER], U8, align_bytes=64)
        w2_codes = keep.tile([P, FEATURE_TILES, PASSES, P], U32, align_bytes=64)
        w2_scales = keep.tile([P, FEATURE_TILES, PASSES, P], U8, align_bytes=64)
        w3_codes = keep.tile([P, PASSES, D_MODEL], U32, align_bytes=64)
        w3_scales = keep.tile([P, PASSES, D_MODEL], U8, align_bytes=64)
        h2_codes = keep.tile([P, PASSES, TOKENS], U32, align_bytes=64)
        h2_scales = keep.tile([P, PASSES, TOKENS], U8, align_bytes=64)

        identity = keep.tile([P, P], F32)
        make_identity(nc, identity[:])

        chunks = (
            [("h1", 0), ("w2", 0), ("h1", 1)]
            + [("w2", c) for c in range(1, 6)]
            + [("h1", 2), ("w2", 6), ("w2", 7), ("h1", 3), ("w3", 0), ("w3", 1)]
        )
        position = {chunk: i for i, chunk in enumerate(chunks)}
        raw_tiles = {}
        residual = {}
        b3_rows = keep.tile([P, D_MODEL], BF16)

        def load(i):
            if i >= len(chunks):
                return
            kind, c = chunks[i]
            rows = slice(c * CHUNK_ROWS, (c + 1) * CHUNK_ROWS)
            raw = raw_pool.tile([P, ROW_TILES, D_FF], BF16, tag="raw")
            if kind == "h1":
                source = h1_rows[rows, :].rearrange("(r p) k -> p r k", p=P)
            elif kind == "w3":
                source = ffn_w3[rows, :].rearrange("(r p) k -> p r k", p=P)
            else:
                source = ffn_w2[rows, :].rearrange("(p r) k -> p r k", p=P)
            if i < SPLIT_LOADS and kind == "h1":
                for j in range(2):
                    cols = slice(j * D_FF // 2, (j + 1) * D_FF // 2)
                    nc.sync.dma_start(out=raw[:, :, cols], in_=source[:, :, cols])
            elif i < SPLIT_LOADS:
                for r in range(ROW_TILES):
                    nc.sync.dma_start(out=raw[:, r, :], in_=source[:, r, :])
            else:
                nc.sync.dma_start(out=raw[:], in_=source)
            raw_tiles[i] = raw

        x1_raw_of = []

        def residual_of(t):
            half, part = divmod(t, TILES_PER_HALF)
            return residual[half][:, part, :]

        def load_residual():
            x1_raw = raw_pool.tile([P, TOKEN_TILES, D_MODEL], BF16, tag="raw")
            for half in range(HALVES):
                residual_tile = raw_pool.tile([P, TILES_PER_HALF, D_MODEL], F32, tag="raw")
                residual[half] = residual_tile
            nc.sync.dma_start(out=b3_rows[:], in_=ffn_b3.partition_broadcast(P))
            nc.sync.dma_start(out=x1_raw[:], in_=x1_rows.rearrange("(t p) d -> p t d", p=P))
            x1_raw_of.append(x1_raw)

        def add_b3(t):
            x1_raw = x1_raw_of[0]
            nc.gpsimd.tensor_tensor(out=residual_of(t), in0=x1_raw[:, t, :], in1=b3_rows[:], op=ALU.add)

        grouped_of = {}

        def transpose_bank(i, r, j):
            kind, c = chunks[i]
            words = raw_tiles[i][:].rearrange("p r k -> p (r k)").bitcast(F32)
            if i not in grouped_of:
                grouped_tile = grouped_pool.tile([P, ROW_TILES * D_FF], BF16, tag="grouped", align_bytes=64)
                grouped_of[i] = grouped_tile
            grouped_words = grouped_of[i][:].bitcast(F32)
            if kind == "w2":
                target = grouped_words.rearrange(
                    "p (r k i u) -> p k r i u", r=ROW_TILES, k=PASSES, i=P
                )
            else:
                target = grouped_words.rearrange(
                    "p (k r i u) -> p k r i u", r=ROW_TILES, k=PASSES, i=P
                )
            bank = bank_pool.tile([P, 2, 2, P], F32, tag="bank")
            for k in range(2):
                for u in range(2):
                    first = r * WORDS + ((2 * j + k) * 2 + u) * P
                    nc.tensor.transpose(bank[:, k, u, :], words[:, first : first + P], identity[:])
            copy = nc.vector.tensor_copy if i < VECTOR_COPIES and (r + j) % 2 else nc.scalar.copy
            copy(
                out=target[:, 2 * j : 2 * j + 2, r, :, :], in_=bank[:].rearrange("q k u i -> q k i u")
            )

        def quantise_w2(m):
            c, r = divmod(m, ROW_TILES)
            nc.vector.quantize_mx(
                out=w2_codes[:, m, :, :].rearrange("p k o -> p (k o)").bitcast(FP8X4),
                scales=w2_scales[:, m, :, :].rearrange("p k o -> p (k o)"),
                in_=grouped_of[position[("w2", c)]][:, r * D_FF : (r + 1) * D_FF],
            )

        def quantise_moving(kind, c, k):
            grouped = grouped_of[position[(kind, c)]]
            cols = slice(c * CHUNK_ROWS, (c + 1) * CHUNK_ROWS)
            codes, scales = w3_codes[:, k, cols], w3_scales[:, k, cols]
            nc.vector.quantize_mx(
                out=codes.bitcast(FP8X4),
                scales=scales,
                in_=grouped[:, k * CHUNK_ROWS * PACK : (k + 1) * CHUNK_ROWS * PACK],
            )

        idle_words = keep.tile([P, HALF], BF16)
        nc.vector.memset(idle_words[:], 0.0)

        def warm_up(n):
            for k in range(n):
                bank = sums_pool.tile([P, HALF], F32, tag="sums")
                nc.tensor.matmul(bank[:], lhsT=idle_words[:, 0:P], rhs=idle_words[:], start=True, stop=True)

        def quantise_half(kind, c, j):
            if kind == "h1":
                nc.vector.quantize_mx(
                    out=h1_codes[:, c, 2 * j : 2 * j + 2, :].rearrange("p k n -> p (k n)").bitcast(FP8X4),
                    scales=h1_scales[:, c, 2 * j : 2 * j + 2, :].rearrange("p k n -> p (k n)"),
                    in_=grouped_of[position[(kind, c)]][:, j * D_FF : (j + 1) * D_FF],
                )
                return
            quantise_moving(kind, c, 2 * j)
            quantise_moving(kind, c, 2 * j + 1)

        def transpose_w2(c):
            i = position[("w2", c)]
            for r in range(ROW_TILES):
                for j in range(2):
                    transpose_bank(i, r, j)
            load(i + RAW_BUFS)

        def transpose_half(kind, c, j):
            i = position[(kind, c)]
            for r in range(ROW_TILES):
                transpose_bank(i, r, j)
            if j == 1:
                load(i + RAW_BUFS)

        a_bf = keep.tile([P, 1], BF16)
        b_bf = keep.tile([P, 1], BF16)
        b2_bf = keep.tile([P, FEATURE_TILES], BF16)
        gains = keep.tile([P, 2], F32)
        sign_a = keep.tile([P, 1], F32)
        squares = keep.tile([P, 2], F32)
        norm2 = keep.tile([P, 1], F32)
        minus_half = keep.tile([P, 1], F32)
        inv_norm = keep.tile([P, 1], F32)
        cos_sin = keep.tile([P, 2], F32)
        gain = keep.tile([P, 1], F32)
        phase = keep.tile([P, 2], F32)
        sin_cos_now = keep.tile([P, 2], F32)
        terms = keep.tile([P, 2], F32)
        step = keep.tile([P, 1], F32)
        bias = keep.tile([P, FEATURE_TILES], F32)
        bias_turns = keep.tile([P, FEATURE_TILES], F32)

        def wave_constants():
            nc.scalar.dma_start(out=a_bf[:], in_=ffn_a2w1.partition_broadcast(P))
            nc.scalar.dma_start(out=b_bf[:], in_=ffn_a2w2.partition_broadcast(P))
            nc.gpsimd.memset(minus_half[:], -0.5)
            nc.scalar.activation(out=step[:], in_=minus_half[:], func=ACT.Sin)
            nc.gpsimd.tensor_copy(out=gains[:, 0:1], in_=a_bf[:])
            nc.gpsimd.tensor_copy(out=gains[:, 1:2], in_=b_bf[:])
            nc.gpsimd.tensor_scalar(
                out=sign_a[:], in0=gains[:, 0:1], scalar1=0.0, scalar2=2.0, op0=ALU.is_ge, op1=ALU.mult
            )
            nc.gpsimd.tensor_scalar(
                out=sign_a[:], in0=sign_a[:], scalar1=1.0, scalar2=-1.0, op0=ALU.mult, op1=ALU.add
            )
            nc.gpsimd.tensor_tensor(out=squares[:], in0=gains[:], in1=gains[:], op=ALU.mult)
            nc.gpsimd.tensor_scalar(
                out=norm2[:], in0=squares[:, 0:1], scalar1=TINY, scalar2=squares[:, 1:2],
                op0=ALU.max, op1=ALU.add,
            )
            nc.gpsimd.tensor_tensor(out=inv_norm[:], in0=norm2[:], in1=minus_half[:], op=ALU.pow)
            nc.gpsimd.tensor_tensor(out=inv_norm[:], in0=inv_norm[:], in1=sign_a[:], op=ALU.mult)
            nc.gpsimd.tensor_scalar(
                out=cos_sin[:], in0=gains[:], scalar1=inv_norm[:, 0:1], scalar2=0.0, op0=ALU.mult, op1=ALU.add
            )
            nc.gpsimd.tensor_tensor(out=gain[:], in0=norm2[:], in1=inv_norm[:], op=ALU.mult)
            nc.gpsimd.tensor_copy(out=phase[:, 0:1], in_=cos_sin[:, 1:2])
            nc.gpsimd.tensor_scalar(
                out=phase[:, 1:2], in0=cos_sin[:, 1:2], scalar1=1.0, scalar2=HALF_PI, op0=ALU.mult, op1=ALU.add
            )

        def newton_step():
            nc.scalar.activation(out=sin_cos_now[:], in_=phase[:], func=ACT.Sin)
            nc.gpsimd.tensor_tensor(out=terms[:], in0=sin_cos_now[:], in1=cos_sin[:], op=ALU.mult)
            nc.gpsimd.tensor_tensor(out=step[:], in0=terms[:, 0:1], in1=terms[:, 1:2], op=ALU.subtract)
            nc.gpsimd.tensor_scalar(
                out=phase[:], in0=phase[:], scalar1=step[:, 0:1], scalar2=0.0, op0=ALU.subtract, op1=ALU.add
            )

        def biases():
            nc.gpsimd.tensor_scalar(
                out=bias[:], in0=b2_bf[:], scalar1=phase[:, 0:1], scalar2=0.0, op0=ALU.add, op1=ALU.add
            )
            nc.gpsimd.tensor_scalar(
                out=bias_turns[:], in0=bias[:], scalar1=1.0 / TWO_PI, scalar2=0.0, op0=ALU.mult, op1=ALU.add
            )

        sums_of = {}
        turns_of = {}
        angle_of = {}
        h2_of = {}
        acc_of = {}

        def bank_of(u, m):
            first, width, group = UNITS[u]
            bank, place = divmod(m % PACK, HALF // width)
            return (u, bank), slice(place * width, (place + 1) * width)

        def first_product(u, m):
            first, width, group = UNITS[u]
            key, cols = bank_of(u, m)
            if key not in sums_of:
                sums_tile = sums_pool.tile([P, HALF], F32, tag="sums")
                sums_of[key] = sums_tile
            for n in range(width // QUARTER):
                q = first // QUARTER + n
                for k in range(PASSES):
                    nc.tensor.matmul_mx(
                        out=sums_of[key][:, cols.start + n * QUARTER : cols.start + (n + 1) * QUARTER],
                        lhsT=w2_codes[:, m, k, :].bitcast(FP8X4),
                        lhsT_scale=w2_scales[:, m, k, :],
                        rhs=h1_codes[:, q, k, :].bitcast(FP8X4),
                        rhs_scale=h1_scales[:, q, k, :],
                        start=(k == 0),
                        stop=(k == PASSES - 1),
                    )

        def count_turns(u, m):
            key, cols = bank_of(u, m)
            if key not in turns_of:
                turns_tile = turns_pool.tile([P, HALF], I32, tag="turns")
                turns_of[key] = turns_tile
            nc.vector.tensor_scalar(
                out=turns_of[key][:, cols], in0=sums_of[key][:, cols], scalar1=1.0 / TWO_PI,
                scalar2=bias_turns[:, m : m + 1], op0=ALU.mult, op1=ALU.add,
            )

        def take_off_turns(u, bank):
            first, width, group = UNITS[u]
            places = slice(bank * (HALF // width), (bank + 1) * (HALF // width))
            if u not in angle_of:
                angle_tile = angle_pool.tile([P, PACK, width], F32, tag="angle%d" % width, bufs=UNIT_BUFS[width][0])
                angle_of[u] = angle_tile
            nc.vector.scalar_tensor_tensor(
                out=angle_of[u][:, places, :].rearrange("p t n -> p (t n)"),
                in0=turns_of[(u, bank)][:], scalar=-TWO_PI,
                in1=sums_of[(u, bank)][:], op0=ALU.mult, op1=ALU.add,
            )

        def sine(u, m):
            angle = angle_of[u]
            nc.scalar.activation(
                out=angle[:, m % PACK, :], in_=angle[:, m % PACK, :], func=ACT.Sin, bias=bias[:, m : m + 1]
            )

        def regroup(u, part, engine):
            first, width, group = UNITS[u]
            if u not in h2_of:
                h2_tile = h2_pool.tile([P, width, PACK], BF16, tag="h2%d" % width, bufs=UNIT_BUFS[width][1], align_bytes=64)
                h2_of[u] = h2_tile
            sines = angle_of[u][:].rearrange("p t (c i) -> p c t i", i=RUN)
            words = h2_of[u][:].rearrange("p (c i) t -> p c t i", i=RUN)
            runs = slice(part * P // RUN, (part + 1) * P // RUN)
            if engine == "S":
                nc.scalar.activation(
                    out=words[:, runs, :, :], in_=sines[:, runs, :, :], func=ACT.Copy, scale=gain[:, 0:1]
                )
            elif engine == "V":
                nc.vector.tensor_scalar_mul(words[:, runs, :, :], sines[:, runs, :, :], gain[:, 0:1])
            else:
                tokens = slice(part * P, (part + 1) * P)
                nc.gpsimd.tensor_scalar(
                    out=h2_of[u][:, tokens, :],
                    in0=angle_of[u][:, :, tokens].rearrange("p t n -> p n t"),
                    scalar1=gain[:, 0:1], scalar2=0.0, op0=ALU.mult, op1=ALU.add,
                )

        def quantise_h2(u):
            first, width, group = UNITS[u]
            step = P if u == len(UNITS) - 1 else width
            for n in range(0, width, step):
                nc.vector.quantize_mx(
                    out=h2_codes[:, group, first + n : first + n + step].bitcast(FP8X4),
                    scales=h2_scales[:, group, first + n : first + n + step],
                    in_=h2_of[u][:, n : n + step, :].rearrange("p n t -> p (n t)"),
                )

        def second_product(t, group):
            cols = slice(t * P, (t + 1) * P)
            if group == 0:
                acc_tile = bank_pool.tile([P, D_MODEL], F32, tag="bank")
                acc_of[t] = acc_tile
            nc.tensor.matmul_mx(
                out=acc_of[t][:],
                lhsT=h2_codes[:, group, cols].bitcast(FP8X4),
                lhsT_scale=h2_scales[:, group, cols],
                rhs=w3_codes[:, group, :].bitcast(FP8X4),
                rhs_scale=w3_scales[:, group, :],
                start=(group == 0),
                stop=(group == PASSES - 1),
            )

        def finish(t):
            nc.vector.tensor_tensor(
                out=residual_of(t), in0=acc_of[t][:], in1=residual_of(t), op=ALU.add
            )
            nc.sync.dma_start(out=out_rows[t * P : (t + 1) * P, :], in_=residual_of(t))

        for i in range(RAW_BUFS):
            load(i)
            if i == 2:
                nc.sync.dma_start(
                    out=b2_bf[:].rearrange("p (c e) -> p c e", e=2),
                    in_=ffn_b2.rearrange("(c p e) -> p c e", p=P, e=2),
                )
        wave_constants()
        warm_up(7)
        transpose_half("h1", 0, 0)
        warm_up(3)
        quantise_half("h1", 0, 0)
        transpose_half("h1", 0, 1)
        warm_up(3)
        quantise_half("h1", 0, 1)
        newton_step()
        transpose_w2(0)
        warm_up(3)
        quantise_w2(0)
        newton_step()
        transpose_half("h1", 1, 0)
        warm_up(3)
        quantise_w2(1)
        quantise_half("h1", 1, 0)
        newton_step()
        transpose_half("h1", 1, 1)
        warm_up(3)
        quantise_half("h1", 1, 1)
        biases()

        rounds = [
            (u, range(PACK * g + first, PACK * g + first + n))
            for u, (token, width, g) in enumerate(UNITS)
            for n in (PACK * QUARTER // width,)
            for first in range(0, PACK, n)
        ]
        products = len(rounds)
        last_product = {u: r for r, (u, tiles) in enumerate(rounds)}

        halves_at = {5: [("h1", 2, 0)], 6: [("h1", 2, 1)], 8: [("h1", 3, 0), ("h1", 3, 1)], 9: [("w3", 0, 0), ("w3", 0, 1)], 10: [("w3", 1, 0)], 11: [("w3", 1, 1)]}
        parts = [(u, part) for u, (token, width, g) in enumerate(UNITS) for part in range(width // P)]
        passes = [(t, u) for u, (token, width, g) in enumerate(UNITS) for t in range(token // P, (token + width) // P)]
        done = {"parts": 0, "units": 0, "passes": 0, "tiles": 0}

        def regroup_parts(r, engines):
            for engine in engines:
                if done["parts"] == len(parts):
                    return
                u, part = parts[done["parts"]]
                if last_product[u] + (2 if UNITS[u][1] == HALF else 1) > r:
                    return
                regroup(u, part, engine)
                done["parts"] += 1

        def quantise_units(r, limit):
            for n in range(limit):
                u = done["units"]
                if u == len(UNITS) or parts.index((u, UNITS[u][1] // P - 1)) >= done["parts"]:
                    return
                quantise_h2(u)
                done["units"] += 1

        def run_passes(limit):
            for n in range(limit):
                if done["passes"] == len(passes):
                    return
                t, u = passes[done["passes"]]
                if u >= done["units"]:
                    return
                second_product(t, UNITS[u][2])
                if UNITS[u][2] == PASSES - 1:
                    complete.append(t)
                done["passes"] += 1

        complete = []

        def finish_tiles():
            for t in complete[done["tiles"] :]:
                finish(t)
                done["tiles"] += 1

        for r in range(ROUNDS):
            if r + 1 < W2_CHUNKS:
                transpose_w2(r + 1)
            if r >= W2_CHUNKS:
                for half in halves_at.get(r, []):
                    transpose_half(*half)
            quantise_units(r, 3)
            if r + 1 < W2_CHUNKS:
                for m in range(ROW_TILES * (r + 1), ROW_TILES * (r + 2)):
                    quantise_w2(m)
            for kind, c, j in halves_at.get(r - 1, []):
                quantise_half(kind, c, j)
            if r == 6:
                load_residual()
            if 8 <= r < 8 + TOKEN_TILES:
                add_b3(r - 8)
            if r < products:
                u, tiles = rounds[r]
                run_passes({14: 4}.get(r, 0))
                for m in tiles:
                    first_product(u, m)
                    if r < W2_CHUNKS and m == tiles[0]:
                        for half in halves_at.get(r, []):
                            transpose_half(*half)
                run_passes({12: 6, 13: 4, 15: 4}.get(r, 0))
                for m in tiles:
                    count_turns(u, m)
                for bank in (0, 1) if len(tiles) == PACK else (tiles[0] % PACK, tiles[1] % PACK):
                    take_off_turns(u, bank)
            finish_tiles()
            if 1 <= r <= products:
                u, tiles = rounds[r - 1]
                for m in tiles:
                    sine(u, m)
            regroup_parts(r, "GV" if r < 6 else "GG" if r < W2_CHUNKS else "GSS" if r < products else "SVSV")
            if r >= products:
                run_passes(len(passes))
        assert done["tiles"] == TOKEN_TILES
